import numpy as np
import ml_dtypes


def mxq(x, axis, fmt="e4m3"):
    dtype, down = {"e4m3": (ml_dtypes.float8_e4m3fn, 7), "e5m2": (ml_dtypes.float8_e5m2, 14)}[fmt]
    v = np.moveaxis(np.asarray(x, np.float32).astype(ml_dtypes.bfloat16).astype(np.float64), axis, -1)
    blocks = v.reshape(v.shape[:-1] + (-1, 32))
    amax = np.abs(blocks).max(-1, keepdims=True)
    byte = np.maximum(np.where(amax > 0, np.frexp(amax)[1] - 1 + 127, 0) - down, 1)
    scale = np.exp2(byte - 127.0)
    codes = (blocks / scale).astype(np.float32).astype(dtype).astype(np.float64)
    return np.moveaxis((codes * scale).reshape(v.shape), -1, axis)


WIDE = False


def mx_kscale(k):
    if not WIDE:
        return np.ones(k)
    levels = np.array([10, -10, 5, -5, 0])
    if k % 512:
        return np.exp2(np.random.permutation(np.resize(levels, k // 32))).repeat(32)
    a = np.empty((k // 512, 16))
    for p in range(k // 512):
        a[p, :8] = np.random.permutation(np.resize(levels, 8))
        for g in range(8):
            far = levels[np.abs(levels - a[p, g]) >= 10]
            a[p, g + 8] = far[np.random.randint(len(far))]
    return np.exp2(a.ravel()).repeat(32)


BF16 = ml_dtypes.bfloat16


def bf(x):
    return np.asarray(x, np.float32).astype(BF16)


def f64(x):
    return np.asarray(x).astype(np.float64)


S, D, N_HEADS, N_KV_HEADS, HEAD_DIM = 8192, 512, 2, 1, 64
Q_DIM = N_HEADS * HEAD_DIM
KV_DIM = N_KV_HEADS * HEAD_DIM
ROPE_THETA = 500000.0


def apply_rope(t, cos, sin):
    te = t[:, :, ::2]
    to = t[:, :, 1::2]
    c = cos[:, None, :]
    s = sin[:, None, :]
    te_rot = te * c - to * s
    to_rot = te * s + to * c
    return np.stack([te_rot, to_rot], axis=-1).reshape(t.shape)


def setup_inputs():
    s = mx_kscale(D)
    inv_freq = 1.0 / ROPE_THETA ** (np.arange(0, HEAD_DIM, 2) / HEAD_DIM)
    angles = np.arange(S)[:, None] * inv_freq[None, :]
    return {"x": bf(np.random.standard_normal((S, D)) * s),
            "freqs_cos": bf(np.cos(angles)),
            "freqs_sin": bf(np.sin(angles)),
            "wqkv": bf(np.random.standard_normal((Q_DIM + 2 * KV_DIM, D)) / np.sqrt(D) / s[None, :])}


def reference(x, freqs_cos, freqs_sin, wqkv):
    qkv = mxq(f64(x), 1, "e4m3") @ mxq(f64(wqkv), 1, "e4m3").T
    q = qkv[:, :Q_DIM].reshape(S, N_HEADS, HEAD_DIM)
    k = qkv[:, Q_DIM:Q_DIM + KV_DIM].reshape(S, N_KV_HEADS, HEAD_DIM)
    v = qkv[:, Q_DIM + KV_DIM:].reshape(S, N_KV_HEADS, HEAD_DIM)
    cos, sin = f64(freqs_cos), f64(freqs_sin)
    return apply_rope(q, cos, sin), apply_rope(k, cos, sin), v

@@ -1,0 +1,230 @@
+from contextlib import ExitStack
+
+import concourse.mybir as mybir
+from concourse.masks import make_identity
+
+F32 = mybir.dt.float32
+BF16 = mybir.dt.bfloat16
+U32 = mybir.dt.uint32
+U8 = mybir.dt.uint8
+FP8X4 = mybir.dt.float8_e4m3fn_x4
+MULT = mybir.AluOpType.mult
+ADD = mybir.AluOpType.add
+
+P = 128
+S = 8192
+D = 512
+WORDS = D // 2
+HEAD = 64
+PAIRS = HEAD // 2
+ROPE_HEADS = 3
+BLOCK = 2 * HEAD
+N_BLOCKS = ROPE_HEADS + 1
+TILES = S // P
+GROUP = 4
+N_GROUPS = TILES // GROUP
+STORE_GROUPS = 2
+
+FLOPS = 2 * S * D * 4 * HEAD
+
+
+def transpose_rows(nc, bank, slot, words, first_word, ident):
+    for u in range(2):
+        nc.tensor.transpose(
+            bank[:, slot, u, :],
+            words[:, first_word + u : first_word + 2 * P : 2],
+            ident[:],
+        )
+
+
+def tile_mha_pa_t_kernel(tc, x, freqs_cos, freqs_sin, wqkv, out_0, out_1, out_2):
+    nc = tc.nc
+
+    x_rows = x.rearrange("(p t) k -> p (t k)", t=TILES)
+    q_rows = out_0.rearrange("(p t) h d -> p t (h d)", t=TILES)
+    k_rows = out_1.rearrange("(p t) h d -> p t (h d)", t=TILES)
+    v_rows = out_2.rearrange("(p t) h d -> p t (h d)", t=TILES)
+
+    with ExitStack() as ctx:
+        const = ctx.enter_context(tc.tile_pool(name="const", bufs=1))
+        x_pool = ctx.enter_context(tc.tile_pool(name="x_pool", bufs=N_GROUPS))
+        quant = ctx.enter_context(tc.tile_pool(name="quant", bufs=3))
+        work = ctx.enter_context(tc.tile_pool(name="work", bufs=3))
+        outs = ctx.enter_context(tc.tile_pool(name="outs", bufs=3))
+        psum_t = ctx.enter_context(tc.psum_pool(name="psum_t", bufs=4))
+        psum_mx = ctx.enter_context(tc.psum_pool(name="psum_mx", bufs=1))
+        ctx.enter_context(tc.manual_schedule())
+
+        w_rows = const.tile([P, 4 * D], BF16)
+        nc.scalar.dma_start(
+            out=w_rows[:, 0 : 2 * D].rearrange("p (a k) -> p a k", a=2),
+            in_=wqkv.rearrange("(a p) k -> p a k", p=P),
+        )
+        nc.scalar.dma_start(
+            out=w_rows[:, 2 * D : 4 * D], in_=wqkv.rearrange("(i e) k -> i (e k)", e=2)
+        )
+        cos_sb = const.tile([P, TILES * PAIRS], BF16)
+        sin_sb = const.tile([P, TILES * PAIRS], BF16)
+        nc.scalar.dma_start(out=cos_sb[:], in_=freqs_cos.rearrange("(p t) i -> p (t i)", t=TILES))
+        nc.scalar.dma_start(out=sin_sb[:], in_=freqs_sin.rearrange("(p t) i -> p (t i)", t=TILES))
+
+        x_tiles = []
+        for g in range(N_GROUPS):
+            x_sb = x_pool.tile([P, GROUP * D], BF16, name="x_sb")
+            nc.sync.dma_start(out=x_sb[:], in_=x_rows[:, g * GROUP * D : (g + 1) * GROUP * D])
+            x_tiles.append(x_sb)
+
+        ident = const.tile([P, P], F32)
+        make_identity(nc, ident[:])
+
+        nc.vector.tensor_scalar_mul(
+            out=w_rows[:, 3 * D : 4 * D], in0=w_rows[:, 3 * D : 4 * D], scalar1=-1.0
+        )
+        w_words = w_rows[:].bitcast(F32)
+        w_plain = psum_t.tile([P, 2, 2, P], F32, tag="bank_t")
+        w_pairs = psum_t.tile([P, 2, 2, P], F32, tag="bank_t")
+        for a in range(2):
+            transpose_rows(nc, w_plain, a, w_words, a * WORDS, ident)
+        for e in range(2):
+            transpose_rows(nc, w_pairs, e, w_words, (2 + e) * WORDS, ident)
+
+        w_grouped = const.tile([P, N_BLOCKS * BLOCK * 4], BF16, align_bytes=64)
+        nc.vector.memset(w_grouped[:, (N_BLOCKS * BLOCK - HEAD) * 4 :], 0.0)
+        w_cols = w_grouped[:].bitcast(F32).rearrange(
+            "p (b s c u) -> p b s c u", b=N_BLOCKS, s=2, u=2
+        )
+        for a in range(2):
+            nc.vector.tensor_copy(
+                out=w_cols[:, 2 * a : 2 * a + 2, 0, :, :],
+                in_=w_plain[:, a, :, :].rearrange("p u (b c) -> p b c u", b=2),
+            )
+        for e in range(2):
+            nc.vector.tensor_copy(
+                out=w_cols[:, 0:ROPE_HEADS, 1, :, :].rearrange(
+                    "p b (i f) u -> p b i f u", f=2
+                )[:, :, :, 1 - e, :],
+                in_=w_pairs[:, e, :, 0 : ROPE_HEADS * PAIRS].rearrange(
+                    "p u (b i) -> p b i u", b=ROPE_HEADS
+                ),
+            )
+        w_codes = const.tile([P, N_BLOCKS * BLOCK], U32, align_bytes=64)
+        w_scales = const.tile([P, N_BLOCKS * BLOCK], U8, align_bytes=64)
+        nc.vector.quantize_mx(out=w_codes[:].bitcast(FP8X4), scales=w_scales[:], in_=w_grouped[:])
+
+        cos_sin = const.tile([P, TILES, 2, PAIRS], BF16)
+        nc.vector.tensor_copy(
+            out=cos_sin[:, :, 0, :], in_=cos_sb[:].rearrange("p (t i) -> p t i", i=PAIRS)
+        )
+        nc.vector.tensor_copy(
+            out=cos_sin[:, :, 1, :], in_=sin_sb[:].rearrange("p (t i) -> p t i", i=PAIRS)
+        )
+
+        grouped_of = {}
+        codes_of = {}
+        banks_of = {}
+        out_tiles = {}
+
+        def transpose_group(g):
+            x_words = x_tiles[g][:].bitcast(F32)
+            grouped = quant.tile([P, GROUP * P * 4], BF16, align_bytes=64, name="grouped")
+            grouped_words = grouped[:].bitcast(F32).rearrange(
+                "p (j r u) -> p j r u", j=GROUP, u=2
+            )
+            banks = []
+            for half in range(GROUP // 2):
+                bank_t = psum_t.tile([P, 2, 2, P], F32, tag="bank_t", name="bank_t")
+                for j in range(2):
+                    transpose_rows(nc, bank_t, j, x_words, (2 * half + j) * WORDS, ident)
+                banks.append(bank_t)
+            for half in range(GROUP // 2):
+                nc.scalar.copy(
+                    out=grouped_words[:, 2 * half : 2 * half + 2, :, :],
+                    in_=banks[half][:].rearrange("p j u r -> p j r u"),
+                )
+            grouped_of[g] = grouped
+
+        def quantise_group(g):
+            codes = quant.tile([P, GROUP * P], U32, align_bytes=64, name="codes")
+            scales = quant.tile([P, GROUP * P], U8, align_bytes=64, name="scales")
+            nc.vector.quantize_mx(
+                out=codes[:].bitcast(FP8X4), scales=scales[:], in_=grouped_of[g][:]
+            )
+            codes_of[g] = (codes, scales)
+
+        def multiply_block(g, b):
+            codes, scales = codes_of[g]
+            bank = psum_mx.tile([P, GROUP, BLOCK], F32, tag="bank_%d" % b, name="bank_%d" % b)
+            for j in range(GROUP):
+                nc.tensor.matmul_mx(
+                    out=bank[:, j, :],
+                    lhsT=codes[:, j * P : (j + 1) * P].bitcast(FP8X4),
+                    lhsT_scale=scales[:, j * P : (j + 1) * P],
+                    rhs=w_codes[:, b * BLOCK : (b + 1) * BLOCK].bitcast(FP8X4),
+                    rhs_scale=w_scales[:, b * BLOCK : (b + 1) * BLOCK],
+                    start=True,
+                    stop=True,
+                )
+            banks_of[(g, b)] = bank
+
+        def products(g, b, prod):
+            table = cos_sin[:, g * GROUP : (g + 1) * GROUP, :, :].rearrange("p t s i -> p t (s i)")
+            nc.vector.tensor_tensor(
+                out=prod[:, b, :, :].rearrange("p j (c f) -> p j c f", f=2),
+                in0=banks_of[(g, b)][:].rearrange("p j (c f) -> p j c f", f=2),
+                in1=table.unsqueeze(3).to_broadcast([P, GROUP, 2 * PAIRS, 2]),
+                op=MULT,
+            )
+
+        def finish_group(g, prod):
+            q_sb, k_sb, v_sb = out_tiles[g // STORE_GROUPS]
+            first = (g % STORE_GROUPS) * GROUP
+            halves = prod[:].rearrange("p b j (s c) -> p j b s c", s=2)
+            nc.gpsimd.tensor_tensor(
+                out=q_sb[:, first : first + GROUP, :].rearrange("p j (b c) -> p j b c", b=2),
+                in0=halves[:, :, 0:2, 0, :],
+                in1=halves[:, :, 0:2, 1, :],
+                op=ADD,
+            )
+            nc.gpsimd.tensor_tensor(
+                out=k_sb[:, first : first + GROUP, :],
+                in0=halves[:, :, 2, 0, :],
+                in1=halves[:, :, 2, 1, :],
+                op=ADD,
+            )
+            if g % STORE_GROUPS == STORE_GROUPS - 1:
+                tiles = slice((g + 1 - STORE_GROUPS) * GROUP, (g + 1) * GROUP)
+                nc.sync.dma_start(out=v_rows[:, tiles, :], in_=v_sb[:])
+                nc.sync.dma_start(out=k_rows[:, tiles, :], in_=k_sb[:])
+                nc.sync.dma_start(out=q_rows[:, tiles, :], in_=q_sb[:])
+
+        def copy_v(g):
+            if g % STORE_GROUPS == 0:
+                q_sb = outs.tile([P, STORE_GROUPS * GROUP, 2 * HEAD], F32, name="q_sb")
+                k_sb = outs.tile([P, STORE_GROUPS * GROUP, HEAD], F32, name="k_sb")
+                v_sb = outs.tile([P, STORE_GROUPS * GROUP, HEAD], F32, name="v_sb")
+                out_tiles[g // STORE_GROUPS] = (q_sb, k_sb, v_sb)
+            v_sb = out_tiles[g // STORE_GROUPS][2]
+            first = (g % STORE_GROUPS) * GROUP
+            nc.scalar.copy(
+                out=v_sb[:, first : first + GROUP, :],
+                in_=banks_of[(g, ROPE_HEADS)][:, :, 0:HEAD],
+            )
+
+        for i in range(N_GROUPS + 2):
+            rotating = 0 <= i - 2
+            multiplying = 0 <= i - 1 < N_GROUPS
+            if rotating:
+                copy_v(i - 2)
+                prod = work.tile([P, ROPE_HEADS, GROUP, BLOCK], F32, name="prod")
+            if i < N_GROUPS:
+                transpose_group(i)
+            if multiplying:
+                quantise_group(i - 1)
+                multiply_block(i - 1, ROPE_HEADS)
+            for b in range(ROPE_HEADS):
+                if rotating:
+                    products(i - 2, b, prod)
+                if multiplying:
+                    multiply_block(i - 1, b)
+            if rotating:
+                finish_group(i - 2, prod)

@@ -10,6 +10,7 @@ U8 = mybir.dt.uint8
 FP8X4 = mybir.dt.float8_e4m3fn_x4
 MULT = mybir.AluOpType.mult
 ADD = mybir.AluOpType.add
+COPY = mybir.ActivationFunctionType.Copy
 
 P = 128
 S = 8192
@@ -18,14 +19,16 @@ WORDS = D // 2
 HEAD = 64
 PAIRS = HEAD // 2
 ROPE_HEADS = 3
-BLOCK = 2 * HEAD
-N_BLOCKS = ROPE_HEADS + 1
+HALF = ROPE_HEADS * PAIRS
+OUT_COLS = 4 * HEAD
 TILES = S // P
+BANK = 2
 GROUP = 4
 N_GROUPS = TILES // GROUP
-STORE_GROUPS = 2
+STORE_TILES = 8
+TABLE_TILES = 16
 
-FLOPS = 2 * S * D * 4 * HEAD
+FLOPS = 2 * S * D * OUT_COLS
 
 
 def transpose_rows(nc, bank, slot, words, first_word, ident):
@@ -41,6 +44,8 @@ def tile_mha_pa_t_kernel(tc, x, freqs_cos, freqs_sin, wqkv, out_0, out_1, out_2)
     nc = tc.nc
 
     x_rows = x.rearrange("(p t) k -> p (t k)", t=TILES)
+    cos_rows = freqs_cos.rearrange("(p t) i -> p t i", t=TILES)
+    sin_rows = freqs_sin.rearrange("(p t) i -> p t i", t=TILES)
     q_rows = out_0.rearrange("(p t) h d -> p t (h d)", t=TILES)
     k_rows = out_1.rearrange("(p t) h d -> p t (h d)", t=TILES)
     v_rows = out_2.rearrange("(p t) h d -> p t (h d)", t=TILES)
@@ -50,96 +55,99 @@ def tile_mha_pa_t_kernel(tc, x, freqs_cos, freqs_sin, wqkv, out_0, out_1, out_2)
         x_pool = ctx.enter_context(tc.tile_pool(name="x_pool", bufs=N_GROUPS))
         quant = ctx.enter_context(tc.tile_pool(name="quant", bufs=3))
         work = ctx.enter_context(tc.tile_pool(name="work", bufs=3))
-        outs = ctx.enter_context(tc.tile_pool(name="outs", bufs=3))
+        outs = ctx.enter_context(tc.tile_pool(name="outs", bufs=TILES // STORE_TILES))
         psum_t = ctx.enter_context(tc.psum_pool(name="psum_t", bufs=4))
-        psum_mx = ctx.enter_context(tc.psum_pool(name="psum_mx", bufs=1))
+        psum_mx = ctx.enter_context(tc.psum_pool(name="psum_mx", bufs=4))
         ctx.enter_context(tc.manual_schedule())
 
-        w_rows = const.tile([P, 4 * D], BF16)
-        nc.scalar.dma_start(
-            out=w_rows[:, 0 : 2 * D].rearrange("p (a k) -> p a k", a=2),
+        w_rows = const.tile([P, 2 * D], BF16)
+        cos_sb = const.tile([P, TILES, PAIRS], BF16)
+        sin_sb = const.tile([P, TILES, PAIRS], BF16)
+        x_tiles = []
+
+        def load_tables(n):
+            tiles = slice(n * TABLE_TILES, (n + 1) * TABLE_TILES)
+            nc.sync.dma_start(out=sin_sb[:, tiles, :], in_=sin_rows[:, tiles, :])
+            nc.sync.dma_start(out=cos_sb[:, tiles, :], in_=cos_rows[:, tiles, :])
+
+        def load_x(g, pieces):
+            x_sb = x_pool.tile([P, GROUP * D], BF16, name="x_sb")
+            width = GROUP * D // pieces
+            for n in range(pieces):
+                nc.sync.dma_start(
+                    out=x_sb[:, n * width : (n + 1) * width],
+                    in_=x_rows[:, g * GROUP * D + n * width : g * GROUP * D + (n + 1) * width],
+                )
+            x_tiles.append(x_sb)
+
+        nc.sync.dma_start(
+            out=w_rows[:].rearrange("p (a k) -> p a k", a=2),
             in_=wqkv.rearrange("(a p) k -> p a k", p=P),
         )
-        nc.scalar.dma_start(
-            out=w_rows[:, 2 * D : 4 * D], in_=wqkv.rearrange("(i e) k -> i (e k)", e=2)
-        )
-        cos_sb = const.tile([P, TILES * PAIRS], BF16)
-        sin_sb = const.tile([P, TILES * PAIRS], BF16)
-        nc.scalar.dma_start(out=cos_sb[:], in_=freqs_cos.rearrange("(p t) i -> p (t i)", t=TILES))
-        nc.scalar.dma_start(out=sin_sb[:], in_=freqs_sin.rearrange("(p t) i -> p (t i)", t=TILES))
-
-        x_tiles = []
         for g in range(N_GROUPS):
-            x_sb = x_pool.tile([P, GROUP * D], BF16, name="x_sb")
-            nc.sync.dma_start(out=x_sb[:], in_=x_rows[:, g * GROUP * D : (g + 1) * GROUP * D])
-            x_tiles.append(x_sb)
+            load_x(g, 2 if g == 0 else 1)
+            if g % 4 == 0:
+                load_tables(g // 4)
 
         ident = const.tile([P, P], F32)
         make_identity(nc, ident[:])
 
-        nc.vector.tensor_scalar_mul(
-            out=w_rows[:, 3 * D : 4 * D], in0=w_rows[:, 3 * D : 4 * D], scalar1=-1.0
-        )
         w_words = w_rows[:].bitcast(F32)
-        w_plain = psum_t.tile([P, 2, 2, P], F32, tag="bank_t")
-        w_pairs = psum_t.tile([P, 2, 2, P], F32, tag="bank_t")
+        w_bank = psum_t.tile([P, BANK, 2, P], F32, tag="bank_t", name="bank_t")
         for a in range(2):
-            transpose_rows(nc, w_plain, a, w_words, a * WORDS, ident)
-        for e in range(2):
-            transpose_rows(nc, w_pairs, e, w_words, (2 + e) * WORDS, ident)
-
-        w_grouped = const.tile([P, N_BLOCKS * BLOCK * 4], BF16, align_bytes=64)
-        nc.vector.memset(w_grouped[:, (N_BLOCKS * BLOCK - HEAD) * 4 :], 0.0)
-        w_cols = w_grouped[:].bitcast(F32).rearrange(
-            "p (b s c u) -> p b s c u", b=N_BLOCKS, s=2, u=2
+            transpose_rows(nc, w_bank, a, w_words, a * WORDS, ident)
+        w_grouped = const.tile([P, OUT_COLS * 4], BF16, align_bytes=64)
+        w_cols = w_grouped[:].bitcast(F32).rearrange("p (c u) -> p c u", u=2)
+        w_halves = w_cols[:, 0 : 2 * HALF, :].rearrange("p (f m) u -> p f m u", f=2)
+        nc.vector.tensor_copy(
+            out=w_halves[:, :, 0:HEAD, :],
+            in_=w_bank[:, 0, :, :].rearrange("p u (m f) -> p f m u", f=2),
         )
-        for a in range(2):
-            nc.vector.tensor_copy(
-                out=w_cols[:, 2 * a : 2 * a + 2, 0, :, :],
-                in_=w_plain[:, a, :, :].rearrange("p u (b c) -> p b c u", b=2),
-            )
-        for e in range(2):
-            nc.vector.tensor_copy(
-                out=w_cols[:, 0:ROPE_HEADS, 1, :, :].rearrange(
-                    "p b (i f) u -> p b i f u", f=2
-                )[:, :, :, 1 - e, :],
-                in_=w_pairs[:, e, :, 0 : ROPE_HEADS * PAIRS].rearrange(
-                    "p u (b i) -> p b i u", b=ROPE_HEADS
-                ),
-            )
-        w_codes = const.tile([P, N_BLOCKS * BLOCK], U32, align_bytes=64)
-        w_scales = const.tile([P, N_BLOCKS * BLOCK], U8, align_bytes=64)
+        nc.vector.tensor_copy(
+            out=w_halves[:, :, HEAD:HALF, :],
+            in_=w_bank[:, 1, :, 0:HEAD].rearrange("p u (m f) -> p f m u", f=2),
+        )
+        nc.vector.tensor_copy(
+            out=w_cols[:, 2 * HALF : OUT_COLS, :],
+            in_=w_bank[:, 1, :, HEAD:P].rearrange("p u c -> p c u"),
+        )
+        w_codes = const.tile([P, OUT_COLS], U32, align_bytes=64)
+        w_scales = const.tile([P, OUT_COLS], U8, align_bytes=64)
         nc.vector.quantize_mx(out=w_codes[:].bitcast(FP8X4), scales=w_scales[:], in_=w_grouped[:])
 
-        cos_sin = const.tile([P, TILES, 2, PAIRS], BF16)
-        nc.vector.tensor_copy(
-            out=cos_sin[:, :, 0, :], in_=cos_sb[:].rearrange("p (t i) -> p t i", i=PAIRS)
-        )
-        nc.vector.tensor_copy(
-            out=cos_sin[:, :, 1, :], in_=sin_sb[:].rearrange("p (t i) -> p t i", i=PAIRS)
-        )
+        signed_sin = const.tile([P, TILES, 2, PAIRS], BF16)
 
+        def sign_tables(n):
+            tiles = slice(n * TABLE_TILES, (n + 1) * TABLE_TILES)
+            nc.scalar.activation(
+                out=signed_sin[:, tiles, 0, :], in_=sin_sb[:, tiles, :], func=COPY, scale=-1.0
+            )
+            nc.scalar.copy(out=signed_sin[:, tiles, 1, :], in_=sin_sb[:, tiles, :])
+
+        banks_t = {}
         grouped_of = {}
         codes_of = {}
         banks_of = {}
         out_tiles = {}
+        products_of = {}
 
         def transpose_group(g):
             x_words = x_tiles[g][:].bitcast(F32)
-            grouped = quant.tile([P, GROUP * P * 4], BF16, align_bytes=64, name="grouped")
-            grouped_words = grouped[:].bitcast(F32).rearrange(
-                "p (j r u) -> p j r u", j=GROUP, u=2
-            )
             banks = []
-            for half in range(GROUP // 2):
-                bank_t = psum_t.tile([P, 2, 2, P], F32, tag="bank_t", name="bank_t")
-                for j in range(2):
-                    transpose_rows(nc, bank_t, j, x_words, (2 * half + j) * WORDS, ident)
+            for n in range(GROUP // BANK):
+                bank_t = psum_t.tile([P, BANK, 2, P], F32, tag="bank_t", name="bank_t")
+                for j in range(BANK):
+                    transpose_rows(nc, bank_t, j, x_words, (BANK * n + j) * WORDS, ident)
                 banks.append(bank_t)
-            for half in range(GROUP // 2):
+            banks_t[g] = banks
+
+        def interleave_group(g):
+            grouped = quant.tile([P, GROUP * P * 4], BF16, align_bytes=64, name="grouped")
+            words = grouped[:].bitcast(F32).rearrange("p (j r u) -> p j r u", j=GROUP, u=2)
+            for n, bank_t in enumerate(banks_t[g]):
                 nc.scalar.copy(
-                    out=grouped_words[:, 2 * half : 2 * half + 2, :, :],
-                    in_=banks[half][:].rearrange("p j u r -> p j r u"),
+                    out=words[:, BANK * n : BANK * (n + 1), :, :],
+                    in_=bank_t[:].rearrange("p j u r -> p j r u"),
                 )
             grouped_of[g] = grouped
 
@@ -151,80 +159,102 @@ def tile_mha_pa_t_kernel(tc, x, freqs_cos, freqs_sin, wqkv, out_0, out_1, out_2)
             )
             codes_of[g] = (codes, scales)
 
-        def multiply_block(g, b):
+        def multiply_group(g):
             codes, scales = codes_of[g]
-            bank = psum_mx.tile([P, GROUP, BLOCK], F32, tag="bank_%d" % b, name="bank_%d" % b)
-            for j in range(GROUP):
-                nc.tensor.matmul_mx(
-                    out=bank[:, j, :],
-                    lhsT=codes[:, j * P : (j + 1) * P].bitcast(FP8X4),
-                    lhsT_scale=scales[:, j * P : (j + 1) * P],
-                    rhs=w_codes[:, b * BLOCK : (b + 1) * BLOCK].bitcast(FP8X4),
-                    rhs_scale=w_scales[:, b * BLOCK : (b + 1) * BLOCK],
-                    start=True,
-                    stop=True,
-                )
-            banks_of[(g, b)] = bank
-
-        def products(g, b, prod):
-            table = cos_sin[:, g * GROUP : (g + 1) * GROUP, :, :].rearrange("p t s i -> p t (s i)")
-            nc.vector.tensor_tensor(
-                out=prod[:, b, :, :].rearrange("p j (c f) -> p j c f", f=2),
-                in0=banks_of[(g, b)][:].rearrange("p j (c f) -> p j c f", f=2),
-                in1=table.unsqueeze(3).to_broadcast([P, GROUP, 2 * PAIRS, 2]),
-                op=MULT,
-            )
-
-        def finish_group(g, prod):
-            q_sb, k_sb, v_sb = out_tiles[g // STORE_GROUPS]
-            first = (g % STORE_GROUPS) * GROUP
-            halves = prod[:].rearrange("p b j (s c) -> p j b s c", s=2)
-            nc.gpsimd.tensor_tensor(
-                out=q_sb[:, first : first + GROUP, :].rearrange("p j (b c) -> p j b c", b=2),
-                in0=halves[:, :, 0:2, 0, :],
-                in1=halves[:, :, 0:2, 1, :],
-                op=ADD,
-            )
-            nc.gpsimd.tensor_tensor(
-                out=k_sb[:, first : first + GROUP, :],
-                in0=halves[:, :, 2, 0, :],
-                in1=halves[:, :, 2, 1, :],
-                op=ADD,
-            )
-            if g % STORE_GROUPS == STORE_GROUPS - 1:
-                tiles = slice((g + 1 - STORE_GROUPS) * GROUP, (g + 1) * GROUP)
-                nc.sync.dma_start(out=v_rows[:, tiles, :], in_=v_sb[:])
-                nc.sync.dma_start(out=k_rows[:, tiles, :], in_=k_sb[:])
-                nc.sync.dma_start(out=q_rows[:, tiles, :], in_=q_sb[:])
+            banks = []
+            for n in range(GROUP // BANK):
+                bank = psum_mx.tile([P, BANK, OUT_COLS], F32, tag="bank_mx", name="bank_mx")
+                for j in range(BANK):
+                    rows = slice((BANK * n + j) * P, (BANK * n + j + 1) * P)
+                    nc.tensor.matmul_mx(
+                        out=bank[:, j, :],
+                        lhsT=codes[:, rows].bitcast(FP8X4),
+                        lhsT_scale=scales[:, rows],
+                        rhs=w_codes[:].bitcast(FP8X4),
+                        rhs_scale=w_scales[:],
+                        start=True,
+                        stop=True,
+                    )
+                banks.append(bank)
+            banks_of[g] = banks
 
         def copy_v(g):
-            if g % STORE_GROUPS == 0:
-                q_sb = outs.tile([P, STORE_GROUPS * GROUP, 2 * HEAD], F32, name="q_sb")
-                k_sb = outs.tile([P, STORE_GROUPS * GROUP, HEAD], F32, name="k_sb")
-                v_sb = outs.tile([P, STORE_GROUPS * GROUP, HEAD], F32, name="v_sb")
-                out_tiles[g // STORE_GROUPS] = (q_sb, k_sb, v_sb)
-            v_sb = out_tiles[g // STORE_GROUPS][2]
-            first = (g % STORE_GROUPS) * GROUP
-            nc.scalar.copy(
-                out=v_sb[:, first : first + GROUP, :],
-                in_=banks_of[(g, ROPE_HEADS)][:, :, 0:HEAD],
-            )
+            n_set, first = divmod(g * GROUP, STORE_TILES)
+            if first == 0:
+                q_sb = outs.tile([P, STORE_TILES, 2 * HEAD], F32, name="q_sb")
+                k_sb = outs.tile([P, STORE_TILES, HEAD], F32, name="k_sb")
+                v_sb = outs.tile([P, STORE_TILES, HEAD], F32, name="v_sb")
+                out_tiles[n_set] = (q_sb, k_sb, v_sb)
+            v_sb = out_tiles[n_set][2]
+            for n, bank in enumerate(banks_of[g]):
+                nc.scalar.copy(
+                    out=v_sb[:, first + BANK * n : first + BANK * (n + 1), :],
+                    in_=bank[:, :, 2 * HALF : OUT_COLS],
+                )
 
-        for i in range(N_GROUPS + 2):
-            rotating = 0 <= i - 2
-            multiplying = 0 <= i - 1 < N_GROUPS
-            if rotating:
-                copy_v(i - 2)
-                prod = work.tile([P, ROPE_HEADS, GROUP, BLOCK], F32, name="prod")
-            if i < N_GROUPS:
-                transpose_group(i)
-            if multiplying:
-                quantise_group(i - 1)
-                multiply_block(i - 1, ROPE_HEADS)
-            for b in range(ROPE_HEADS):
-                if rotating:
-                    products(i - 2, b, prod)
-                if multiplying:
-                    multiply_block(i - 1, b)
-            if rotating:
-                finish_group(i - 2, prod)
+        def multiply_tables(g):
+            by_cos = work.tile([P, GROUP, 2, HALF], F32, name="by_cos")
+            by_sin = work.tile([P, GROUP, 2, HALF], F32, name="by_sin")
+            shape = [P, BANK, 2, ROPE_HEADS, PAIRS]
+            for n, bank in enumerate(banks_of[g]):
+                here = slice(BANK * n, BANK * (n + 1))
+                tiles = slice(g * GROUP + BANK * n, g * GROUP + BANK * (n + 1))
+                halves = bank[:, :, 0 : 2 * HALF].rearrange(
+                    "p j (f h i) -> p j f h i", f=2, h=ROPE_HEADS
+                )
+                nc.vector.tensor_tensor(
+                    out=by_cos[:, here, :, :].rearrange("p j f (h i) -> p j (f h) i", i=PAIRS),
+                    in0=bank[:, :, 0 : 2 * HALF].rearrange("p j (b i) -> p j b i", i=PAIRS),
+                    in1=cos_sb[:, tiles, :]
+                    .unsqueeze(2)
+                    .to_broadcast([P, BANK, 2 * ROPE_HEADS, PAIRS]),
+                    op=MULT,
+                )
+                nc.vector.tensor_tensor(
+                    out=by_sin[:, here, :, :].rearrange("p j f (h i) -> p j f h i", i=PAIRS),
+                    in0=halves[:, :, ::-1, :, :],
+                    in1=signed_sin[:, tiles, :, :].unsqueeze(3).to_broadcast(shape),
+                    op=MULT,
+                )
+            products_of[g] = (by_cos, by_sin)
+
+        def add_group(g):
+            by_cos, by_sin = products_of[g]
+            n_set, first = divmod(g * GROUP, STORE_TILES)
+            q_sb, k_sb, v_sb = out_tiles[n_set]
+            here = slice(first, first + GROUP)
+            for out_sb, cols in ((q_sb, slice(0, HEAD)), (k_sb, slice(HEAD, HALF))):
+                nc.gpsimd.tensor_tensor(
+                    out=out_sb[:, here, :].rearrange("p j (m f) -> p j m f", f=2),
+                    in0=by_cos[:, :, :, cols].rearrange("p j f m -> p j m f"),
+                    in1=by_sin[:, :, :, cols].rearrange("p j f m -> p j m f"),
+                    op=ADD,
+                )
+            if first + GROUP == STORE_TILES:
+                tiles = slice(n_set * STORE_TILES, (n_set + 1) * STORE_TILES)
+                nc.sync.dma_start(out=v_rows[:, tiles, :], in_=v_sb[:])
+                nc.sync.dma_start(out=q_rows[:, tiles, :], in_=q_sb[:])
+                nc.sync.dma_start(out=k_rows[:, tiles, :], in_=k_sb[:])
+
+        transpose_group(0)
+        interleave_group(0)
+        sign_tables(0)
+        quantise_group(0)
+        transpose_group(1)
+        for g in range(N_GROUPS + 1):
+            if g < N_GROUPS:
+                multiply_group(g)
+            if g + 2 < N_GROUPS:
+                transpose_group(g + 2)
+            if g + 1 < N_GROUPS:
+                interleave_group(g + 1)
+            if g < N_GROUPS:
+                copy_v(g)
+            if g >= 1:
+                multiply_tables(g - 1)
+            if g + 1 < N_GROUPS:
+                quantise_group(g + 1)
+            if g % 4 == 2 and g + 2 < N_GROUPS:
+                sign_tables(g // 4 + 1)
+            if g >= 1:
+                add_group(g - 1)

@@ -19,7 +19,7 @@ WORDS = D // 2
 HEAD = 64
 PAIRS = HEAD // 2
 ROPE_HEADS = 3
-HALF = ROPE_HEADS * PAIRS
+ROPE_COLS = ROPE_HEADS * HEAD
 OUT_COLS = 4 * HEAD
 TILES = S // P
 BANK = 2
@@ -98,18 +98,9 @@ def tile_mha_pa_t_kernel(tc, x, freqs_cos, freqs_sin, wqkv, out_0, out_1, out_2)
             transpose_rows(nc, w_bank, a, w_words, a * WORDS, ident)
         w_grouped = const.tile([P, OUT_COLS * 4], BF16, align_bytes=64)
         w_cols = w_grouped[:].bitcast(F32).rearrange("p (c u) -> p c u", u=2)
-        w_halves = w_cols[:, 0 : 2 * HALF, :].rearrange("p (f m) u -> p f m u", f=2)
         nc.vector.tensor_copy(
-            out=w_halves[:, :, 0:HEAD, :],
-            in_=w_bank[:, 0, :, :].rearrange("p u (m f) -> p f m u", f=2),
-        )
-        nc.vector.tensor_copy(
-            out=w_halves[:, :, HEAD:HALF, :],
-            in_=w_bank[:, 1, :, 0:HEAD].rearrange("p u (m f) -> p f m u", f=2),
-        )
-        nc.vector.tensor_copy(
-            out=w_cols[:, 2 * HALF : OUT_COLS, :],
-            in_=w_bank[:, 1, :, HEAD:P].rearrange("p u c -> p c u"),
+            out=w_cols.rearrange("p (a r) u -> p a r u", a=2),
+            in_=w_bank[:].rearrange("p a u r -> p a r u"),
         )
         w_codes = const.tile([P, OUT_COLS], U32, align_bytes=64)
         w_scales = const.tile([P, OUT_COLS], U8, align_bytes=64)
@@ -189,31 +180,31 @@ def tile_mha_pa_t_kernel(tc, x, freqs_cos, freqs_sin, wqkv, out_0, out_1, out_2)
             for n, bank in enumerate(banks_of[g]):
                 nc.scalar.copy(
                     out=v_sb[:, first + BANK * n : first + BANK * (n + 1), :],
-                    in_=bank[:, :, 2 * HALF : OUT_COLS],
+                    in_=bank[:, :, ROPE_COLS:OUT_COLS],
                 )
 
         def multiply_tables(g):
-            by_cos = work.tile([P, GROUP, 2, HALF], F32, name="by_cos")
-            by_sin = work.tile([P, GROUP, 2, HALF], F32, name="by_sin")
-            shape = [P, BANK, 2, ROPE_HEADS, PAIRS]
-            for n, bank in enumerate(banks_of[g]):
-                here = slice(BANK * n, BANK * (n + 1))
-                tiles = slice(g * GROUP + BANK * n, g * GROUP + BANK * (n + 1))
-                halves = bank[:, :, 0 : 2 * HALF].rearrange(
-                    "p j (f h i) -> p j f h i", f=2, h=ROPE_HEADS
+            by_cos = work.tile([P, GROUP, ROPE_COLS], F32, name="by_cos")
+            by_sin = work.tile([P, GROUP, ROPE_COLS], F32, name="by_sin")
+            shape = [P, ROPE_HEADS, PAIRS, 2]
+            for j in range(GROUP):
+                pairs = banks_of[g][j // BANK][:, j % BANK, 0:ROPE_COLS].rearrange(
+                    "p (h i f) -> p h i f", h=ROPE_HEADS, f=2
                 )
+                t = g * GROUP + j
                 nc.vector.tensor_tensor(
-                    out=by_cos[:, here, :, :].rearrange("p j f (h i) -> p j (f h) i", i=PAIRS),
-                    in0=bank[:, :, 0 : 2 * HALF].rearrange("p j (b i) -> p j b i", i=PAIRS),
-                    in1=cos_sb[:, tiles, :]
-                    .unsqueeze(2)
-                    .to_broadcast([P, BANK, 2 * ROPE_HEADS, PAIRS]),
+                    out=by_cos[:, j, :].rearrange("p (h i f) -> p h i f", h=ROPE_HEADS, f=2),
+                    in0=pairs,
+                    in1=cos_sb[:, t, :].unsqueeze(1).unsqueeze(3).to_broadcast(shape),
                     op=MULT,
                 )
                 nc.vector.tensor_tensor(
-                    out=by_sin[:, here, :, :].rearrange("p j f (h i) -> p j f h i", i=PAIRS),
-                    in0=halves[:, :, ::-1, :, :],
-                    in1=signed_sin[:, tiles, :, :].unsqueeze(3).to_broadcast(shape),
+                    out=by_sin[:, j, :].rearrange("p (h i f) -> p h i f", h=ROPE_HEADS, f=2),
+                    in0=pairs[:, :, :, ::-1],
+                    in1=signed_sin[:, t, :, :]
+                    .rearrange("p f i -> p i f")
+                    .unsqueeze(1)
+                    .to_broadcast(shape),
                     op=MULT,
                 )
             products_of[g] = (by_cos, by_sin)
@@ -223,12 +214,9 @@ def tile_mha_pa_t_kernel(tc, x, freqs_cos, freqs_sin, wqkv, out_0, out_1, out_2)
             n_set, first = divmod(g * GROUP, STORE_TILES)
             q_sb, k_sb, v_sb = out_tiles[n_set]
             here = slice(first, first + GROUP)
-            for out_sb, cols in ((q_sb, slice(0, HEAD)), (k_sb, slice(HEAD, HALF))):
+            for out_sb, cols in ((q_sb, slice(0, 2 * HEAD)), (k_sb, slice(2 * HEAD, ROPE_COLS))):
                 nc.gpsimd.tensor_tensor(
-                    out=out_sb[:, here, :].rearrange("p j (m f) -> p j m f", f=2),
-                    in0=by_cos[:, :, :, cols].rearrange("p j f m -> p j m f"),
-                    in1=by_sin[:, :, :, cols].rearrange("p j f m -> p j m f"),
-                    op=ADD,
+                    out=out_sb[:, here, :], in0=by_cos[:, :, cols], in1=by_sin[:, :, cols], op=ADD
                 )
             if first + GROUP == STORE_TILES:
                 tiles = slice(n_set * STORE_TILES, (n_set + 1) * STORE_TILES)

@@ -23,10 +23,14 @@ ROPE_COLS = ROPE_HEADS * HEAD
 OUT_COLS = 4 * HEAD
 TILES = S // P
 BANK = 2
-GROUP = 4
-N_GROUPS = TILES // GROUP
-STORE_TILES = 8
-TABLE_TILES = 16
+GROUP_TILES = (2, 2) + (4,) * 14 + (2, 2)
+N_GROUPS = len(GROUP_TILES)
+FIRST_TILE = tuple(sum(GROUP_TILES[:g]) for g in range(N_GROUPS))
+MAX_GROUP = max(GROUP_TILES)
+STORE_TILES = (8,) * 7 + (4, 2, 2)
+STORE_END = tuple(sum(STORE_TILES[: n + 1]) for n in range(len(STORE_TILES)))
+TABLE_TILES = (8, 24, 32)
+DRAIN_GROUPS = 2
 
 FLOPS = 2 * S * D * OUT_COLS
 
@@ -52,10 +56,10 @@ def tile_mha_pa_t_kernel(tc, x, freqs_cos, freqs_sin, wqkv, out_0, out_1, out_2)
 
     with ExitStack() as ctx:
         const = ctx.enter_context(tc.tile_pool(name="const", bufs=1))
-        x_pool = ctx.enter_context(tc.tile_pool(name="x_pool", bufs=N_GROUPS))
+        x_pool = ctx.enter_context(tc.tile_pool(name="x_pool", bufs=1))
         quant = ctx.enter_context(tc.tile_pool(name="quant", bufs=3))
         work = ctx.enter_context(tc.tile_pool(name="work", bufs=3))
-        outs = ctx.enter_context(tc.tile_pool(name="outs", bufs=TILES // STORE_TILES))
+        outs = ctx.enter_context(tc.tile_pool(name="outs", bufs=1))
         psum_t = ctx.enter_context(tc.psum_pool(name="psum_t", bufs=4))
         psum_mx = ctx.enter_context(tc.psum_pool(name="psum_mx", bufs=4))
         ctx.enter_context(tc.manual_schedule())
@@ -66,18 +70,14 @@ def tile_mha_pa_t_kernel(tc, x, freqs_cos, freqs_sin, wqkv, out_0, out_1, out_2)
         x_tiles = []
 
         def load_tables(n):
-            tiles = slice(n * TABLE_TILES, (n + 1) * TABLE_TILES)
+            tiles = slice(sum(TABLE_TILES[:n]), sum(TABLE_TILES[: n + 1]))
             nc.sync.dma_start(out=sin_sb[:, tiles, :], in_=sin_rows[:, tiles, :])
             nc.sync.dma_start(out=cos_sb[:, tiles, :], in_=cos_rows[:, tiles, :])
 
-        def load_x(g, pieces):
-            x_sb = x_pool.tile([P, GROUP * D], BF16, name="x_sb")
-            width = GROUP * D // pieces
-            for n in range(pieces):
-                nc.sync.dma_start(
-                    out=x_sb[:, n * width : (n + 1) * width],
-                    in_=x_rows[:, g * GROUP * D + n * width : g * GROUP * D + (n + 1) * width],
-                )
+        def load_x(g):
+            x_sb = x_pool.tile([P, GROUP_TILES[g] * D], BF16, name="x_sb", tag="x_%d" % g)
+            first = FIRST_TILE[g] * D
+            nc.sync.dma_start(out=x_sb[:], in_=x_rows[:, first : first + GROUP_TILES[g] * D])
             x_tiles.append(x_sb)
 
         nc.sync.dma_start(
@@ -85,9 +85,13 @@ def tile_mha_pa_t_kernel(tc, x, freqs_cos, freqs_sin, wqkv, out_0, out_1, out_2)
             in_=wqkv.rearrange("(a p) k -> p a k", p=P),
         )
         for g in range(N_GROUPS):
-            load_x(g, 2 if g == 0 else 1)
-            if g % 4 == 0:
-                load_tables(g // 4)
+            load_x(g)
+            if g == 0:
+                load_tables(0)
+            if g == 2:
+                load_tables(1)
+            if g == 5:
+                load_tables(2)
 
         ident = const.tile([P, P], F32)
         make_identity(nc, ident[:])
@@ -108,8 +112,14 @@ def tile_mha_pa_t_kernel(tc, x, freqs_cos, freqs_sin, wqkv, out_0, out_1, out_2)
 
         signed_sin = const.tile([P, TILES, 2, PAIRS], BF16)
 
-        def sign_tables(n):
-            tiles = slice(n * TABLE_TILES, (n + 1) * TABLE_TILES)
+        tiles = slice(0, TABLE_TILES[0])
+        nc.vector.tensor_scalar_mul(
+            out=signed_sin[:, tiles, 0, :], in0=sin_sb[:, tiles, :], scalar1=-1.0
+        )
+        nc.vector.tensor_copy(out=signed_sin[:, tiles, 1, :], in_=sin_sb[:, tiles, :])
+
+        def sign_tables(first, end):
+            tiles = slice(first, end)
             nc.scalar.activation(
                 out=signed_sin[:, tiles, 0, :], in_=sin_sb[:, tiles, :], func=COPY, scale=-1.0
             )
@@ -122,38 +132,41 @@ def tile_mha_pa_t_kernel(tc, x, freqs_cos, freqs_sin, wqkv, out_0, out_1, out_2)
         out_tiles = {}
         products_of = {}
 
+        def banks_in(g):
+            return range(GROUP_TILES[g] // BANK)
+
         def transpose_group(g):
             x_words = x_tiles[g][:].bitcast(F32)
-            banks = []
-            for n in range(GROUP // BANK):
+            for n in banks_in(g):
                 bank_t = psum_t.tile([P, BANK, 2, P], F32, tag="bank_t", name="bank_t")
                 for j in range(BANK):
                     transpose_rows(nc, bank_t, j, x_words, (BANK * n + j) * WORDS, ident)
-                banks.append(bank_t)
-            banks_t[g] = banks
+                banks_t[(g, n)] = bank_t
 
         def interleave_group(g):
-            grouped = quant.tile([P, GROUP * P * 4], BF16, align_bytes=64, name="grouped")
-            words = grouped[:].bitcast(F32).rearrange("p (j r u) -> p j r u", j=GROUP, u=2)
-            for n, bank_t in enumerate(banks_t[g]):
+            grouped = quant.tile([P, MAX_GROUP * P * 4], BF16, align_bytes=64, name="grouped")
+            words = grouped[:].bitcast(F32).rearrange("p (j r u) -> p j r u", r=P, u=2)
+            for n in banks_in(g):
                 nc.scalar.copy(
                     out=words[:, BANK * n : BANK * (n + 1), :, :],
-                    in_=bank_t[:].rearrange("p j u r -> p j r u"),
+                    in_=banks_t[(g, n)][:].rearrange("p j u r -> p j r u"),
                 )
             grouped_of[g] = grouped
 
         def quantise_group(g):
-            codes = quant.tile([P, GROUP * P], U32, align_bytes=64, name="codes")
-            scales = quant.tile([P, GROUP * P], U8, align_bytes=64, name="scales")
+            cols = GROUP_TILES[g] * P
+            codes = quant.tile([P, MAX_GROUP * P], U32, align_bytes=64, name="codes")
+            scales = quant.tile([P, MAX_GROUP * P], U8, align_bytes=64, name="scales")
             nc.vector.quantize_mx(
-                out=codes[:].bitcast(FP8X4), scales=scales[:], in_=grouped_of[g][:]
+                out=codes[:, 0:cols].bitcast(FP8X4),
+                scales=scales[:, 0:cols],
+                in_=grouped_of[g][:, 0 : 4 * cols],
             )
             codes_of[g] = (codes, scales)
 
         def multiply_group(g):
             codes, scales = codes_of[g]
-            banks = []
-            for n in range(GROUP // BANK):
+            for n in banks_in(g):
                 bank = psum_mx.tile([P, BANK, OUT_COLS], F32, tag="bank_mx", name="bank_mx")
                 for j in range(BANK):
                     rows = slice((BANK * n + j) * P, (BANK * n + j + 1) * P)
@@ -166,32 +179,35 @@ def tile_mha_pa_t_kernel(tc, x, freqs_cos, freqs_sin, wqkv, out_0, out_1, out_2)
                         start=True,
                         stop=True,
                     )
-                banks.append(bank)
-            banks_of[g] = banks
+                banks_of[(g, n)] = bank
+
+        def place_of(tile):
+            n_set = sum(end <= tile for end in STORE_END)
+            return n_set, tile - (STORE_END[n_set] - STORE_TILES[n_set])
 
         def copy_v(g):
-            n_set, first = divmod(g * GROUP, STORE_TILES)
+            n_set, first = place_of(FIRST_TILE[g])
             if first == 0:
-                q_sb = outs.tile([P, STORE_TILES, 2 * HEAD], F32, name="q_sb")
-                k_sb = outs.tile([P, STORE_TILES, HEAD], F32, name="k_sb")
-                v_sb = outs.tile([P, STORE_TILES, HEAD], F32, name="v_sb")
+                size = STORE_TILES[n_set]
+                q_sb = outs.tile([P, size, 2 * HEAD], F32, name="q_sb", tag="q_%d" % n_set)
+                k_sb = outs.tile([P, size, HEAD], F32, name="k_sb", tag="k_%d" % n_set)
+                v_sb = outs.tile([P, size, HEAD], F32, name="v_sb", tag="v_%d" % n_set)
                 out_tiles[n_set] = (q_sb, k_sb, v_sb)
-            v_sb = out_tiles[n_set][2]
-            for n, bank in enumerate(banks_of[g]):
+            for n in banks_in(g):
                 nc.scalar.copy(
-                    out=v_sb[:, first + BANK * n : first + BANK * (n + 1), :],
-                    in_=bank[:, :, ROPE_COLS:OUT_COLS],
+                    out=out_tiles[n_set][2][:, first + BANK * n : first + BANK * (n + 1), :],
+                    in_=banks_of[(g, n)][:, :, ROPE_COLS:OUT_COLS],
                 )
 
         def multiply_tables(g):
-            by_cos = work.tile([P, GROUP, ROPE_COLS], F32, name="by_cos")
-            by_sin = work.tile([P, GROUP, ROPE_COLS], F32, name="by_sin")
+            by_cos = work.tile([P, MAX_GROUP, ROPE_COLS], F32, name="by_cos")
+            by_sin = work.tile([P, MAX_GROUP, ROPE_COLS], F32, name="by_sin")
             shape = [P, ROPE_HEADS, PAIRS, 2]
-            for j in range(GROUP):
-                pairs = banks_of[g][j // BANK][:, j % BANK, 0:ROPE_COLS].rearrange(
+            for j in range(GROUP_TILES[g]):
+                pairs = banks_of[(g, j // BANK)][:, j % BANK, 0:ROPE_COLS].rearrange(
                     "p (h i f) -> p h i f", h=ROPE_HEADS, f=2
                 )
-                t = g * GROUP + j
+                t = FIRST_TILE[g] + j
                 nc.vector.tensor_tensor(
                     out=by_cos[:, j, :].rearrange("p (h i f) -> p h i f", h=ROPE_HEADS, f=2),
                     in0=pairs,
@@ -210,23 +226,26 @@ def tile_mha_pa_t_kernel(tc, x, freqs_cos, freqs_sin, wqkv, out_0, out_1, out_2)
             products_of[g] = (by_cos, by_sin)
 
         def add_group(g):
+            engine = nc.vector if g >= N_GROUPS - DRAIN_GROUPS else nc.gpsimd
             by_cos, by_sin = products_of[g]
-            n_set, first = divmod(g * GROUP, STORE_TILES)
+            size = GROUP_TILES[g]
+            n_set, first = place_of(FIRST_TILE[g])
             q_sb, k_sb, v_sb = out_tiles[n_set]
-            here = slice(first, first + GROUP)
             for out_sb, cols in ((q_sb, slice(0, 2 * HEAD)), (k_sb, slice(2 * HEAD, ROPE_COLS))):
-                nc.gpsimd.tensor_tensor(
-                    out=out_sb[:, here, :], in0=by_cos[:, :, cols], in1=by_sin[:, :, cols], op=ADD
+                engine.tensor_tensor(
+                    out=out_sb[:, first : first + size, :],
+                    in0=by_cos[:, 0:size, cols],
+                    in1=by_sin[:, 0:size, cols],
+                    op=ADD,
                 )
-            if first + GROUP == STORE_TILES:
-                tiles = slice(n_set * STORE_TILES, (n_set + 1) * STORE_TILES)
+            if first + size == STORE_TILES[n_set]:
+                tiles = slice(STORE_END[n_set] - STORE_TILES[n_set], STORE_END[n_set])
                 nc.sync.dma_start(out=v_rows[:, tiles, :], in_=v_sb[:])
                 nc.sync.dma_start(out=q_rows[:, tiles, :], in_=q_sb[:])
                 nc.sync.dma_start(out=k_rows[:, tiles, :], in_=k_sb[:])
 
         transpose_group(0)
         interleave_group(0)
-        sign_tables(0)
         quantise_group(0)
         transpose_group(1)
         for g in range(N_GROUPS + 1):
@@ -242,7 +261,11 @@ def tile_mha_pa_t_kernel(tc, x, freqs_cos, freqs_sin, wqkv, out_0, out_1, out_2)
                 multiply_tables(g - 1)
             if g + 1 < N_GROUPS:
                 quantise_group(g + 1)
-            if g % 4 == 2 and g + 2 < N_GROUPS:
-                sign_tables(g // 4 + 1)
-            if g >= 1:
+            if g == 2:
+                sign_tables(TABLE_TILES[0], TABLE_TILES[0] + TABLE_TILES[1])
+            if g == 6:
+                sign_tables(TABLE_TILES[0] + TABLE_TILES[1], TILES)
+            if 1 <= g <= N_GROUPS - DRAIN_GROUPS:
                 add_group(g - 1)
+        for g in range(N_GROUPS - DRAIN_GROUPS, N_GROUPS):
+            add_group(g)

@@ -66,12 +66,12 @@ def tile_mha_pa_t_kernel(tc, x, freqs_cos, freqs_sin, wqkv, out_0, out_1, out_2)
 
         w_rows = const.tile([P, 2 * D], BF16)
         cos_sb = const.tile([P, TILES, PAIRS], BF16)
-        sin_sb = const.tile([P, TILES, PAIRS], BF16)
+        signed_sin = const.tile([P, 2, TILES, PAIRS], BF16)
         x_tiles = []
 
         def load_tables(n):
             tiles = slice(sum(TABLE_TILES[:n]), sum(TABLE_TILES[: n + 1]))
-            nc.sync.dma_start(out=sin_sb[:, tiles, :], in_=sin_rows[:, tiles, :])
+            nc.sync.dma_start(out=signed_sin[:, 1, tiles, :], in_=sin_rows[:, tiles, :])
             nc.sync.dma_start(out=cos_sb[:, tiles, :], in_=cos_rows[:, tiles, :])
 
         def load_x(g):
@@ -110,20 +110,11 @@ def tile_mha_pa_t_kernel(tc, x, freqs_cos, freqs_sin, wqkv, out_0, out_1, out_2)
         w_scales = const.tile([P, OUT_COLS], U8, align_bytes=64)
         nc.vector.quantize_mx(out=w_codes[:].bitcast(FP8X4), scales=w_scales[:], in_=w_grouped[:])
 
-        signed_sin = const.tile([P, TILES, 2, PAIRS], BF16)
-
-        tiles = slice(0, TABLE_TILES[0])
         nc.vector.tensor_scalar_mul(
-            out=signed_sin[:, tiles, 0, :], in0=sin_sb[:, tiles, :], scalar1=-1.0
+            out=signed_sin[:, 0, 0 : TABLE_TILES[0], :],
+            in0=signed_sin[:, 1, 0 : TABLE_TILES[0], :],
+            scalar1=-1.0,
         )
-        nc.vector.tensor_copy(out=signed_sin[:, tiles, 1, :], in_=sin_sb[:, tiles, :])
-
-        def sign_tables(first, end):
-            tiles = slice(first, end)
-            nc.scalar.activation(
-                out=signed_sin[:, tiles, 0, :], in_=sin_sb[:, tiles, :], func=COPY, scale=-1.0
-            )
-            nc.scalar.copy(out=signed_sin[:, tiles, 1, :], in_=sin_sb[:, tiles, :])
 
         banks_t = {}
         grouped_of = {}
@@ -131,6 +122,16 @@ def tile_mha_pa_t_kernel(tc, x, freqs_cos, freqs_sin, wqkv, out_0, out_1, out_2)
         banks_of = {}
         out_tiles = {}
         products_of = {}
+
+        def negate_sin(g):
+            if FIRST_TILE[g] >= TABLE_TILES[0]:
+                tiles = slice(FIRST_TILE[g], FIRST_TILE[g] + GROUP_TILES[g])
+                nc.scalar.activation(
+                    out=signed_sin[:, 0, tiles, :],
+                    in_=signed_sin[:, 1, tiles, :],
+                    func=COPY,
+                    scale=-1.0,
+                )
 
         def banks_in(g):
             return range(GROUP_TILES[g] // BANK)
@@ -217,7 +218,7 @@ def tile_mha_pa_t_kernel(tc, x, freqs_cos, freqs_sin, wqkv, out_0, out_1, out_2)
                 nc.vector.tensor_tensor(
                     out=by_sin[:, j, :].rearrange("p (h i f) -> p h i f", h=ROPE_HEADS, f=2),
                     in0=pairs[:, :, :, ::-1],
-                    in1=signed_sin[:, t, :, :]
+                    in1=signed_sin[:, :, t, :]
                     .rearrange("p f i -> p i f")
                     .unsqueeze(1)
                     .to_broadcast(shape),
@@ -225,20 +226,22 @@ def tile_mha_pa_t_kernel(tc, x, freqs_cos, freqs_sin, wqkv, out_0, out_1, out_2)
                 )
             products_of[g] = (by_cos, by_sin)
 
-        def add_group(g):
-            engine = nc.vector if g >= N_GROUPS - DRAIN_GROUPS else nc.gpsimd
+        def add_heads(engine, g, kind):
             by_cos, by_sin = products_of[g]
             size = GROUP_TILES[g]
             n_set, first = place_of(FIRST_TILE[g])
-            q_sb, k_sb, v_sb = out_tiles[n_set]
-            for out_sb, cols in ((q_sb, slice(0, 2 * HEAD)), (k_sb, slice(2 * HEAD, ROPE_COLS))):
-                engine.tensor_tensor(
-                    out=out_sb[:, first : first + size, :],
-                    in0=by_cos[:, 0:size, cols],
-                    in1=by_sin[:, 0:size, cols],
-                    op=ADD,
-                )
-            if first + size == STORE_TILES[n_set]:
+            cols = (slice(0, 2 * HEAD), slice(2 * HEAD, ROPE_COLS))[kind]
+            engine.tensor_tensor(
+                out=out_tiles[n_set][kind][:, first : first + size, :],
+                in0=by_cos[:, 0:size, cols],
+                in1=by_sin[:, 0:size, cols],
+                op=ADD,
+            )
+
+        def store_group(g):
+            n_set, first = place_of(FIRST_TILE[g])
+            if first + GROUP_TILES[g] == STORE_TILES[n_set]:
+                q_sb, k_sb, v_sb = out_tiles[n_set]
                 tiles = slice(STORE_END[n_set] - STORE_TILES[n_set], STORE_END[n_set])
                 nc.sync.dma_start(out=v_rows[:, tiles, :], in_=v_sb[:])
                 nc.sync.dma_start(out=q_rows[:, tiles, :], in_=q_sb[:])
@@ -257,15 +260,19 @@ def tile_mha_pa_t_kernel(tc, x, freqs_cos, freqs_sin, wqkv, out_0, out_1, out_2)
                 interleave_group(g + 1)
             if g < N_GROUPS:
                 copy_v(g)
+            if g + 2 < N_GROUPS:
+                negate_sin(g + 2)
             if g >= 1:
                 multiply_tables(g - 1)
+            if g >= 2:
+                if g - 2 >= N_GROUPS - DRAIN_GROUPS:
+                    add_heads(nc.vector, g - 2, 0)
+                add_heads(nc.vector, g - 2, 1)
+                store_group(g - 2)
             if g + 1 < N_GROUPS:
                 quantise_group(g + 1)
-            if g == 2:
-                sign_tables(TABLE_TILES[0], TABLE_TILES[0] + TABLE_TILES[1])
-            if g == 6:
-                sign_tables(TABLE_TILES[0] + TABLE_TILES[1], TILES)
             if 1 <= g <= N_GROUPS - DRAIN_GROUPS:
-                add_group(g - 1)
-        for g in range(N_GROUPS - DRAIN_GROUPS, N_GROUPS):
-            add_group(g)
+                add_heads(nc.gpsimd, g - 1, 0)
+        add_heads(nc.vector, N_GROUPS - 1, 0)
+        add_heads(nc.vector, N_GROUPS - 1, 1)
+        store_group(N_GROUPS - 1)

@@ -136,13 +136,12 @@ def tile_mha_pa_t_kernel(tc, x, freqs_cos, freqs_sin, wqkv, out_0, out_1, out_2)
         def banks_in(g):
             return range(GROUP_TILES[g] // BANK)
 
-        def transpose_group(g):
+        def transpose_bank(g, n):
             x_words = x_tiles[g][:].bitcast(F32)
-            for n in banks_in(g):
-                bank_t = psum_t.tile([P, BANK, 2, P], F32, tag="bank_t", name="bank_t")
-                for j in range(BANK):
-                    transpose_rows(nc, bank_t, j, x_words, (BANK * n + j) * WORDS, ident)
-                banks_t[(g, n)] = bank_t
+            bank_t = psum_t.tile([P, BANK, 2, P], F32, tag="bank_t", name="bank_t")
+            for j in range(BANK):
+                transpose_rows(nc, bank_t, j, x_words, (BANK * n + j) * WORDS, ident)
+            banks_t[(g, n)] = bank_t
 
         def interleave_group(g):
             grouped = quant.tile([P, MAX_GROUP * P * 4], BF16, align_bytes=64, name="grouped")
@@ -165,22 +164,21 @@ def tile_mha_pa_t_kernel(tc, x, freqs_cos, freqs_sin, wqkv, out_0, out_1, out_2)
             )
             codes_of[g] = (codes, scales)
 
-        def multiply_group(g):
+        def multiply_bank(g, n):
             codes, scales = codes_of[g]
-            for n in banks_in(g):
-                bank = psum_mx.tile([P, BANK, OUT_COLS], F32, tag="bank_mx", name="bank_mx")
-                for j in range(BANK):
-                    rows = slice((BANK * n + j) * P, (BANK * n + j + 1) * P)
-                    nc.tensor.matmul_mx(
-                        out=bank[:, j, :],
-                        lhsT=codes[:, rows].bitcast(FP8X4),
-                        lhsT_scale=scales[:, rows],
-                        rhs=w_codes[:].bitcast(FP8X4),
-                        rhs_scale=w_scales[:],
-                        start=True,
-                        stop=True,
-                    )
-                banks_of[(g, n)] = bank
+            bank = psum_mx.tile([P, BANK, OUT_COLS], F32, tag="bank_mx", name="bank_mx")
+            for j in (0, 0, 1):
+                rows = slice((BANK * n + j) * P, (BANK * n + j + 1) * P)
+                nc.tensor.matmul_mx(
+                    out=bank[:, j, :],
+                    lhsT=codes[:, rows].bitcast(FP8X4),
+                    lhsT_scale=scales[:, rows],
+                    rhs=w_codes[:].bitcast(FP8X4),
+                    rhs_scale=w_scales[:],
+                    start=True,
+                    stop=True,
+                )
+            banks_of[(g, n)] = bank
 
         def place_of(tile):
             n_set = sum(end <= tile for end in STORE_END)
@@ -247,15 +245,16 @@ def tile_mha_pa_t_kernel(tc, x, freqs_cos, freqs_sin, wqkv, out_0, out_1, out_2)
                 nc.sync.dma_start(out=q_rows[:, tiles, :], in_=q_sb[:])
                 nc.sync.dma_start(out=k_rows[:, tiles, :], in_=k_sb[:])
 
-        transpose_group(0)
+        transpose_bank(0, 0)
         interleave_group(0)
         quantise_group(0)
-        transpose_group(1)
+        transpose_bank(1, 0)
         for g in range(N_GROUPS + 1):
-            if g < N_GROUPS:
-                multiply_group(g)
-            if g + 2 < N_GROUPS:
-                transpose_group(g + 2)
+            for n in range(MAX_GROUP // BANK):
+                if g < N_GROUPS and n in banks_in(g):
+                    multiply_bank(g, n)
+                if g + 2 < N_GROUPS and n in banks_in(g + 2):
+                    transpose_bank(g + 2, n)
             if g + 1 < N_GROUPS:
                 interleave_group(g + 1)
             if g < N_GROUPS:

@@ -167,7 +167,7 @@ def tile_mha_pa_t_kernel(tc, x, freqs_cos, freqs_sin, wqkv, out_0, out_1, out_2)
         def multiply_bank(g, n):
             codes, scales = codes_of[g]
             bank = psum_mx.tile([P, BANK, OUT_COLS], F32, tag="bank_mx", name="bank_mx")
-            for j in (0, 0, 1):
+            for j in (0, 0, 1, 1):
                 rows = slice((BANK * n + j) * P, (BANK * n + j + 1) * P)
                 nc.tensor.matmul_mx(
                     out=bank[:, j, :],
@@ -201,27 +201,30 @@ def tile_mha_pa_t_kernel(tc, x, freqs_cos, freqs_sin, wqkv, out_0, out_1, out_2)
         def multiply_tables(g):
             by_cos = work.tile([P, MAX_GROUP, ROPE_COLS], F32, name="by_cos")
             by_sin = work.tile([P, MAX_GROUP, ROPE_COLS], F32, name="by_sin")
-            shape = [P, ROPE_HEADS, PAIRS, 2]
-            for j in range(GROUP_TILES[g]):
-                pairs = banks_of[(g, j // BANK)][:, j % BANK, 0:ROPE_COLS].rearrange(
-                    "p (h i f) -> p h i f", h=ROPE_HEADS, f=2
+            shape = [P, ROPE_HEADS, BANK, PAIRS, 2]
+            for n in banks_in(g):
+                here = slice(BANK * n, BANK * (n + 1))
+                tiles = slice(FIRST_TILE[g] + BANK * n, FIRST_TILE[g] + BANK * (n + 1))
+                pairs = banks_of[(g, n)][:, :, 0:ROPE_COLS].rearrange(
+                    "p j (h i f) -> p h j i f", h=ROPE_HEADS, f=2
                 )
-                t = FIRST_TILE[g] + j
-                nc.vector.tensor_tensor(
-                    out=by_cos[:, j, :].rearrange("p (h i f) -> p h i f", h=ROPE_HEADS, f=2),
-                    in0=pairs,
-                    in1=cos_sb[:, t, :].unsqueeze(1).unsqueeze(3).to_broadcast(shape),
-                    op=MULT,
-                )
-                nc.vector.tensor_tensor(
-                    out=by_sin[:, j, :].rearrange("p (h i f) -> p h i f", h=ROPE_HEADS, f=2),
-                    in0=pairs[:, :, :, ::-1],
-                    in1=signed_sin[:, :, t, :]
-                    .rearrange("p f i -> p i f")
-                    .unsqueeze(1)
-                    .to_broadcast(shape),
-                    op=MULT,
-                )
+                for out_sb, table in (
+                    (by_cos, cos_sb[:, tiles, :].unsqueeze(1).unsqueeze(4)),
+                    (
+                        by_sin,
+                        signed_sin[:, :, tiles, :]
+                        .rearrange("p f t i -> p t i f")[:, :, :, ::-1]
+                        .unsqueeze(1),
+                    ),
+                ):
+                    nc.vector.tensor_tensor(
+                        out=out_sb[:, here, :].rearrange(
+                            "p j (h i f) -> p h j i f", h=ROPE_HEADS, f=2
+                        ),
+                        in0=pairs,
+                        in1=table.to_broadcast(shape),
+                        op=MULT,
+                    )
             products_of[g] = (by_cos, by_sin)
 
         def add_heads(engine, g, kind):
@@ -230,9 +233,11 @@ def tile_mha_pa_t_kernel(tc, x, freqs_cos, freqs_sin, wqkv, out_0, out_1, out_2)
             n_set, first = place_of(FIRST_TILE[g])
             cols = (slice(0, 2 * HEAD), slice(2 * HEAD, ROPE_COLS))[kind]
             engine.tensor_tensor(
-                out=out_tiles[n_set][kind][:, first : first + size, :],
-                in0=by_cos[:, 0:size, cols],
-                in1=by_sin[:, 0:size, cols],
+                out=out_tiles[n_set][kind][:, first : first + size, :].rearrange(
+                    "p j (c f) -> p j c f", f=2
+                ),
+                in0=by_cos[:, 0:size, cols].rearrange("p j (c f) -> p j c f", f=2),
+                in1=by_sin[:, 0:size, cols].rearrange("p j (c f) -> p j c f", f=2)[:, :, :, ::-1],
                 op=ADD,
             )
 

@@ -10,7 +10,6 @@ U8 = mybir.dt.uint8
 FP8X4 = mybir.dt.float8_e4m3fn_x4
 MULT = mybir.AluOpType.mult
 ADD = mybir.AluOpType.add
-COPY = mybir.ActivationFunctionType.Copy
 
 P = 128
 S = 8192
@@ -30,6 +29,8 @@ MAX_GROUP = max(GROUP_TILES)
 STORE_TILES = (8,) * 7 + (4, 2, 2)
 STORE_END = tuple(sum(STORE_TILES[: n + 1]) for n in range(len(STORE_TILES)))
 TABLE_TILES = (8, 24, 32)
+SPLIT_TILES = 3
+FIRST_SPLIT = 5
 DRAIN_GROUPS = 2
 
 FLOPS = 2 * S * D * OUT_COLS
@@ -110,12 +111,15 @@ def tile_mha_pa_t_kernel(tc, x, freqs_cos, freqs_sin, wqkv, out_0, out_1, out_2)
         w_scales = const.tile([P, OUT_COLS], U8, align_bytes=64)
         nc.vector.quantize_mx(out=w_codes[:].bitcast(FP8X4), scales=w_scales[:], in_=w_grouped[:])
 
-        nc.vector.tensor_scalar_mul(
-            out=signed_sin[:, 0, 0 : TABLE_TILES[0], :],
-            in0=signed_sin[:, 1, 0 : TABLE_TILES[0], :],
-            scalar1=-1.0,
-        )
+        def negate_sin(n):
+            tiles = slice(sum(TABLE_TILES[:n]), sum(TABLE_TILES[: n + 1]))
+            nc.vector.tensor_scalar_mul(
+                out=signed_sin[:, 0, tiles, :], in0=signed_sin[:, 1, tiles, :], scalar1=-1.0
+            )
 
+        negate_sin(0)
+
+        halves_of = {}
         banks_t = {}
         grouped_of = {}
         codes_of = {}
@@ -123,24 +127,36 @@ def tile_mha_pa_t_kernel(tc, x, freqs_cos, freqs_sin, wqkv, out_0, out_1, out_2)
         out_tiles = {}
         products_of = {}
 
-        def negate_sin(g):
-            if FIRST_TILE[g] >= TABLE_TILES[0]:
-                tiles = slice(FIRST_TILE[g], FIRST_TILE[g] + GROUP_TILES[g])
-                nc.scalar.activation(
-                    out=signed_sin[:, 0, tiles, :],
-                    in_=signed_sin[:, 1, tiles, :],
-                    func=COPY,
-                    scale=-1.0,
-                )
-
         def banks_in(g):
             return range(GROUP_TILES[g] // BANK)
+
+        def split_tiles(g):
+            return SPLIT_TILES if g >= FIRST_SPLIT and GROUP_TILES[g] == MAX_GROUP else 0
+
+        def split_group(g):
+            n_tiles = split_tiles(g)
+            if n_tiles:
+                halves = quant.tile([P, SPLIT_TILES, 2, P], F32, name="halves")
+                nc.scalar.copy(
+                    out=halves[:],
+                    in_=x_tiles[g][:, 0 : n_tiles * D]
+                    .bitcast(F32)
+                    .rearrange("p (j w u) -> p j u w", j=n_tiles, u=2),
+                )
+                halves_of[g] = halves
 
         def transpose_bank(g, n):
             x_words = x_tiles[g][:].bitcast(F32)
             bank_t = psum_t.tile([P, BANK, 2, P], F32, tag="bank_t", name="bank_t")
             for j in range(BANK):
-                transpose_rows(nc, bank_t, j, x_words, (BANK * n + j) * WORDS, ident)
+                tile = BANK * n + j
+                if tile < split_tiles(g):
+                    for u in range(2):
+                        nc.tensor.transpose(
+                            bank_t[:, j, u, :], halves_of[g][:, tile, u, :], ident[:]
+                        )
+                else:
+                    transpose_rows(nc, bank_t, j, x_words, tile * WORDS, ident)
             banks_t[(g, n)] = bank_t
 
         def interleave_group(g):
@@ -167,7 +183,7 @@ def tile_mha_pa_t_kernel(tc, x, freqs_cos, freqs_sin, wqkv, out_0, out_1, out_2)
         def multiply_bank(g, n):
             codes, scales = codes_of[g]
             bank = psum_mx.tile([P, BANK, OUT_COLS], F32, tag="bank_mx", name="bank_mx")
-            for j in (0, 0, 1, 1):
+            for j in range(BANK):
                 rows = slice((BANK * n + j) * P, (BANK * n + j + 1) * P)
                 nc.tensor.matmul_mx(
                     out=bank[:, j, :],
@@ -255,17 +271,18 @@ def tile_mha_pa_t_kernel(tc, x, freqs_cos, freqs_sin, wqkv, out_0, out_1, out_2)
         quantise_group(0)
         transpose_bank(1, 0)
         for g in range(N_GROUPS + 1):
-            for n in range(MAX_GROUP // BANK):
-                if g < N_GROUPS and n in banks_in(g):
+            if g < N_GROUPS:
+                for n in banks_in(g):
                     multiply_bank(g, n)
-                if g + 2 < N_GROUPS and n in banks_in(g + 2):
+            if g + 2 < N_GROUPS:
+                for n in banks_in(g + 2):
                     transpose_bank(g + 2, n)
             if g + 1 < N_GROUPS:
                 interleave_group(g + 1)
             if g < N_GROUPS:
                 copy_v(g)
-            if g + 2 < N_GROUPS:
-                negate_sin(g + 2)
+            if g + 3 < N_GROUPS:
+                split_group(g + 3)
             if g >= 1:
                 multiply_tables(g - 1)
             if g >= 2:
@@ -275,6 +292,10 @@ def tile_mha_pa_t_kernel(tc, x, freqs_cos, freqs_sin, wqkv, out_0, out_1, out_2)
                 store_group(g - 2)
             if g + 1 < N_GROUPS:
                 quantise_group(g + 1)
+            if g == 2:
+                negate_sin(1)
+            if g == 7:
+                negate_sin(2)
             if 1 <= g <= N_GROUPS - DRAIN_GROUPS:
                 add_heads(nc.gpsimd, g - 1, 0)
         add_heads(nc.vector, N_GROUPS - 1, 0)

@@ -10,6 +10,7 @@ U8 = mybir.dt.uint8
 FP8X4 = mybir.dt.float8_e4m3fn_x4
 MULT = mybir.AluOpType.mult
 ADD = mybir.AluOpType.add
+COPY = mybir.ActivationFunctionType.Copy
 
 P = 128
 S = 8192
@@ -22,16 +23,15 @@ ROPE_COLS = ROPE_HEADS * HEAD
 OUT_COLS = 4 * HEAD
 TILES = S // P
 BANK = 2
-GROUP_TILES = (2, 2) + (4,) * 14 + (2, 2)
+GROUP_TILES = (2,) * 4 + (4,) * 13 + (2, 2)
 N_GROUPS = len(GROUP_TILES)
 FIRST_TILE = tuple(sum(GROUP_TILES[:g]) for g in range(N_GROUPS))
 MAX_GROUP = max(GROUP_TILES)
 STORE_TILES = (8,) * 7 + (4, 2, 2)
 STORE_END = tuple(sum(STORE_TILES[: n + 1]) for n in range(len(STORE_TILES)))
 TABLE_TILES = (8, 24, 32)
-SPLIT_TILES = 3
-FIRST_SPLIT = 5
-DRAIN_GROUPS = 2
+SPLIT_TILES = 2
+FIRST_SPLIT = 8
 
 FLOPS = 2 * S * D * OUT_COLS
 
@@ -89,36 +89,39 @@ def tile_mha_pa_t_kernel(tc, x, freqs_cos, freqs_sin, wqkv, out_0, out_1, out_2)
             load_x(g)
             if g == 0:
                 load_tables(0)
-            if g == 2:
+            if g == 3:
                 load_tables(1)
-            if g == 5:
+            if g == 6:
                 load_tables(2)
 
         ident = const.tile([P, P], F32)
         make_identity(nc, ident[:])
 
         w_words = w_rows[:].bitcast(F32)
-        w_bank = psum_t.tile([P, BANK, 2, P], F32, tag="bank_t", name="bank_t")
+        w_banks = []
         for a in range(2):
-            transpose_rows(nc, w_bank, a, w_words, a * WORDS, ident)
+            w_bank = psum_t.tile([P, BANK, 2, P], F32, tag="bank_t", name="bank_t")
+            transpose_rows(nc, w_bank, 0, w_words, a * WORDS, ident)
+            w_banks.append(w_bank)
         w_grouped = const.tile([P, OUT_COLS * 4], BF16, align_bytes=64)
         w_cols = w_grouped[:].bitcast(F32).rearrange("p (c u) -> p c u", u=2)
         nc.vector.tensor_copy(
-            out=w_cols.rearrange("p (a r) u -> p a r u", a=2),
-            in_=w_bank[:].rearrange("p a u r -> p a r u"),
+            out=w_cols[:, 0:P, :], in_=w_banks[0][:, 0, :, :].rearrange("p u r -> p r u")
+        )
+        nc.scalar.copy(
+            out=w_cols[:, P : 2 * P, :], in_=w_banks[1][:, 0, :, :].rearrange("p u r -> p r u")
         )
         w_codes = const.tile([P, OUT_COLS], U32, align_bytes=64)
         w_scales = const.tile([P, OUT_COLS], U8, align_bytes=64)
         nc.vector.quantize_mx(out=w_codes[:].bitcast(FP8X4), scales=w_scales[:], in_=w_grouped[:])
 
-        def negate_sin(n):
-            tiles = slice(sum(TABLE_TILES[:n]), sum(TABLE_TILES[: n + 1]))
-            nc.vector.tensor_scalar_mul(
-                out=signed_sin[:, 0, tiles, :], in0=signed_sin[:, 1, tiles, :], scalar1=-1.0
-            )
+        nc.vector.tensor_scalar_mul(
+            out=signed_sin[:, 0, 0 : TABLE_TILES[0], :],
+            in0=signed_sin[:, 1, 0 : TABLE_TILES[0], :],
+            scalar1=-1.0,
+        )
 
-        negate_sin(0)
-
+        one_word = const.tile([P, 1], U32)
         halves_of = {}
         banks_t = {}
         grouped_of = {}
@@ -126,6 +129,16 @@ def tile_mha_pa_t_kernel(tc, x, freqs_cos, freqs_sin, wqkv, out_0, out_1, out_2)
         banks_of = {}
         out_tiles = {}
         products_of = {}
+
+        def negate_sin(g):
+            if FIRST_TILE[g] >= TABLE_TILES[0]:
+                tiles = slice(FIRST_TILE[g], FIRST_TILE[g] + GROUP_TILES[g])
+                nc.scalar.activation(
+                    out=signed_sin[:, 0, tiles, :],
+                    in_=signed_sin[:, 1, tiles, :],
+                    func=COPY,
+                    scale=-1.0,
+                )
 
         def banks_in(g):
             return range(GROUP_TILES[g] // BANK)
@@ -159,11 +172,11 @@ def tile_mha_pa_t_kernel(tc, x, freqs_cos, freqs_sin, wqkv, out_0, out_1, out_2)
                     transpose_rows(nc, bank_t, j, x_words, tile * WORDS, ident)
             banks_t[(g, n)] = bank_t
 
-        def interleave_group(g):
+        def interleave_group(g, copy):
             grouped = quant.tile([P, MAX_GROUP * P * 4], BF16, align_bytes=64, name="grouped")
             words = grouped[:].bitcast(F32).rearrange("p (j r u) -> p j r u", r=P, u=2)
             for n in banks_in(g):
-                nc.scalar.copy(
+                copy(
                     out=words[:, BANK * n : BANK * (n + 1), :, :],
                     in_=banks_t[(g, n)][:].rearrange("p j u r -> p j r u"),
                 )
@@ -257,6 +270,9 @@ def tile_mha_pa_t_kernel(tc, x, freqs_cos, freqs_sin, wqkv, out_0, out_1, out_2)
                 op=ADD,
             )
 
+        def wait_for_codes(g):
+            nc.gpsimd.tensor_copy(out=one_word[:], in_=codes_of[g][0][:, 0:1])
+
         def store_group(g):
             n_set, first = place_of(FIRST_TILE[g])
             if first + GROUP_TILES[g] == STORE_TILES[n_set]:
@@ -267,9 +283,11 @@ def tile_mha_pa_t_kernel(tc, x, freqs_cos, freqs_sin, wqkv, out_0, out_1, out_2)
                 nc.sync.dma_start(out=k_rows[:, tiles, :], in_=k_sb[:])
 
         transpose_bank(0, 0)
-        interleave_group(0)
-        quantise_group(0)
         transpose_bank(1, 0)
+        interleave_group(0, nc.scalar.copy)
+        quantise_group(0)
+        interleave_group(1, nc.vector.tensor_copy)
+        quantise_group(1)
         for g in range(N_GROUPS + 1):
             if g < N_GROUPS:
                 for n in banks_in(g):
@@ -277,26 +295,23 @@ def tile_mha_pa_t_kernel(tc, x, freqs_cos, freqs_sin, wqkv, out_0, out_1, out_2)
             if g + 2 < N_GROUPS:
                 for n in banks_in(g + 2):
                     transpose_bank(g + 2, n)
-            if g + 1 < N_GROUPS:
-                interleave_group(g + 1)
-            if g < N_GROUPS:
-                copy_v(g)
+            if 1 <= g < N_GROUPS - 1:
+                interleave_group(g + 1, nc.scalar.copy)
+            if g + 2 < N_GROUPS:
+                negate_sin(g + 2)
             if g + 3 < N_GROUPS:
                 split_group(g + 3)
             if g >= 1:
                 multiply_tables(g - 1)
-            if g >= 2:
-                if g - 2 >= N_GROUPS - DRAIN_GROUPS:
-                    add_heads(nc.vector, g - 2, 0)
+                copy_v(g - 1)
+            if 2 <= g:
                 add_heads(nc.vector, g - 2, 1)
                 store_group(g - 2)
-            if g + 1 < N_GROUPS:
+            if 1 <= g < N_GROUPS - 1:
                 quantise_group(g + 1)
-            if g == 2:
-                negate_sin(1)
-            if g == 7:
-                negate_sin(2)
-            if 1 <= g <= N_GROUPS - DRAIN_GROUPS:
+            if 1 <= g < N_GROUPS:
+                if g + 1 < N_GROUPS:
+                    wait_for_codes(g + 1)
                 add_heads(nc.gpsimd, g - 1, 0)
         add_heads(nc.vector, N_GROUPS - 1, 0)
         add_heads(nc.vector, N_GROUPS - 1, 1)

@@ -81,13 +81,13 @@ def tile_mha_pa_t_kernel(tc, x, freqs_cos, freqs_sin, wqkv, out_0, out_1, out_2)
             nc.sync.dma_start(out=x_sb[:], in_=x_rows[:, first : first + GROUP_TILES[g] * D])
             x_tiles.append(x_sb)
 
-        nc.sync.dma_start(
-            out=w_rows[:].rearrange("p (a k) -> p a k", a=2),
-            in_=wqkv.rearrange("(a p) k -> p a k", p=P),
-        )
         for g in range(N_GROUPS):
             load_x(g)
             if g == 0:
+                nc.sync.dma_start(
+                    out=w_rows[:].rearrange("p (a k) -> p a k", a=2),
+                    in_=wqkv.rearrange("(a p) k -> p a k", p=P),
+                )
                 load_tables(0)
             if g == 3:
                 load_tables(1)
@@ -97,31 +97,9 @@ def tile_mha_pa_t_kernel(tc, x, freqs_cos, freqs_sin, wqkv, out_0, out_1, out_2)
         ident = const.tile([P, P], F32)
         make_identity(nc, ident[:])
 
-        w_words = w_rows[:].bitcast(F32)
-        w_banks = []
-        for a in range(2):
-            w_bank = psum_t.tile([P, BANK, 2, P], F32, tag="bank_t", name="bank_t")
-            transpose_rows(nc, w_bank, 0, w_words, a * WORDS, ident)
-            w_banks.append(w_bank)
-        w_grouped = const.tile([P, OUT_COLS * 4], BF16, align_bytes=64)
-        w_cols = w_grouped[:].bitcast(F32).rearrange("p (c u) -> p c u", u=2)
-        nc.vector.tensor_copy(
-            out=w_cols[:, 0:P, :], in_=w_banks[0][:, 0, :, :].rearrange("p u r -> p r u")
-        )
-        nc.scalar.copy(
-            out=w_cols[:, P : 2 * P, :], in_=w_banks[1][:, 0, :, :].rearrange("p u r -> p r u")
-        )
         w_codes = const.tile([P, OUT_COLS], U32, align_bytes=64)
         w_scales = const.tile([P, OUT_COLS], U8, align_bytes=64)
-        nc.vector.quantize_mx(out=w_codes[:].bitcast(FP8X4), scales=w_scales[:], in_=w_grouped[:])
 
-        nc.vector.tensor_scalar_mul(
-            out=signed_sin[:, 0, 0 : TABLE_TILES[0], :],
-            in0=signed_sin[:, 1, 0 : TABLE_TILES[0], :],
-            scalar1=-1.0,
-        )
-
-        one_word = const.tile([P, 1], U32)
         halves_of = {}
         banks_t = {}
         grouped_of = {}
@@ -270,9 +248,6 @@ def tile_mha_pa_t_kernel(tc, x, freqs_cos, freqs_sin, wqkv, out_0, out_1, out_2)
                 op=ADD,
             )
 
-        def wait_for_codes(g):
-            nc.gpsimd.tensor_copy(out=one_word[:], in_=codes_of[g][0][:, 0:1])
-
         def store_group(g):
             n_set, first = place_of(FIRST_TILE[g])
             if first + GROUP_TILES[g] == STORE_TILES[n_set]:
@@ -282,11 +257,27 @@ def tile_mha_pa_t_kernel(tc, x, freqs_cos, freqs_sin, wqkv, out_0, out_1, out_2)
                 nc.sync.dma_start(out=q_rows[:, tiles, :], in_=q_sb[:])
                 nc.sync.dma_start(out=k_rows[:, tiles, :], in_=k_sb[:])
 
+        w_words = w_rows[:].bitcast(F32)
+        w_grouped = const.tile([P, OUT_COLS * 4], BF16, align_bytes=64)
+        w_cols = w_grouped[:].bitcast(F32).rearrange("p (c u) -> p c u", u=2)
+        w_banks = []
         transpose_bank(0, 0)
+        for a in range(2):
+            w_bank = psum_t.tile([P, BANK, 2, P], F32, tag="bank_t", name="bank_t")
+            transpose_rows(nc, w_bank, 0, w_words, a * WORDS, ident)
+            w_banks.append(w_bank[:, 0, :, :].rearrange("p u r -> p r u"))
         transpose_bank(1, 0)
         interleave_group(0, nc.scalar.copy)
+        nc.vector.tensor_copy(out=w_cols[:, 0:P, :], in_=w_banks[0])
+        nc.scalar.copy(out=w_cols[:, P : 2 * P, :], in_=w_banks[1])
         quantise_group(0)
+        nc.vector.quantize_mx(out=w_codes[:].bitcast(FP8X4), scales=w_scales[:], in_=w_grouped[:])
         interleave_group(1, nc.vector.tensor_copy)
+        nc.vector.tensor_scalar_mul(
+            out=signed_sin[:, 0, 0 : TABLE_TILES[0], :],
+            in0=signed_sin[:, 1, 0 : TABLE_TILES[0], :],
+            scalar1=-1.0,
+        )
         quantise_group(1)
         for g in range(N_GROUPS + 1):
             if g < N_GROUPS:
@@ -301,8 +292,11 @@ def tile_mha_pa_t_kernel(tc, x, freqs_cos, freqs_sin, wqkv, out_0, out_1, out_2)
                 negate_sin(g + 2)
             if g + 3 < N_GROUPS:
                 split_group(g + 3)
+            if g == N_GROUPS - 1:
+                copy_v(g)
             if g >= 1:
                 multiply_tables(g - 1)
+            if 1 <= g < N_GROUPS:
                 copy_v(g - 1)
             if 2 <= g:
                 add_heads(nc.vector, g - 2, 1)
@@ -310,8 +304,6 @@ def tile_mha_pa_t_kernel(tc, x, freqs_cos, freqs_sin, wqkv, out_0, out_1, out_2)
             if 1 <= g < N_GROUPS - 1:
                 quantise_group(g + 1)
             if 1 <= g < N_GROUPS:
-                if g + 1 < N_GROUPS:
-                    wait_for_codes(g + 1)
                 add_heads(nc.gpsimd, g - 1, 0)
         add_heads(nc.vector, N_GROUPS - 1, 0)
         add_heads(nc.vector, N_GROUPS - 1, 1)

from contextlib import ExitStack

import concourse.mybir as mybir
from concourse.masks import make_identity

F32 = mybir.dt.float32
BF16 = mybir.dt.bfloat16
U32 = mybir.dt.uint32
U8 = mybir.dt.uint8
FP8X4 = mybir.dt.float8_e4m3fn_x4
MULT = mybir.AluOpType.mult
ADD = mybir.AluOpType.add
COPY = mybir.ActivationFunctionType.Copy

P = 128
S = 8192
D = 512
WORDS = D // 2
HEAD = 64
PAIRS = HEAD // 2
ROPE_HEADS = 3
ROPE_COLS = ROPE_HEADS * HEAD
OUT_COLS = 4 * HEAD
TILES = S // P
BANK = 2
GROUP_TILES = (2,) * 4 + (4,) * 13 + (2, 2)
N_GROUPS = len(GROUP_TILES)
FIRST_TILE = tuple(sum(GROUP_TILES[:g]) for g in range(N_GROUPS))
MAX_GROUP = max(GROUP_TILES)
STORE_TILES = (8,) * 7 + (4, 2, 2)
STORE_END = tuple(sum(STORE_TILES[: n + 1]) for n in range(len(STORE_TILES)))
TABLE_TILES = (8, 24, 32)
SPLIT_TILES = 2
FIRST_SPLIT = 8

FLOPS = 2 * S * D * OUT_COLS


def transpose_rows(nc, bank, slot, words, first_word, ident):
    for u in range(2):
        nc.tensor.transpose(
            bank[:, slot, u, :],
            words[:, first_word + u : first_word + 2 * P : 2],
            ident[:],
        )


def tile_mha_pa_t_kernel(tc, x, freqs_cos, freqs_sin, wqkv, out_0, out_1, out_2):
    nc = tc.nc

    x_rows = x.rearrange("(p t) k -> p (t k)", t=TILES)
    cos_rows = freqs_cos.rearrange("(p t) i -> p t i", t=TILES)
    sin_rows = freqs_sin.rearrange("(p t) i -> p t i", t=TILES)
    q_rows = out_0.rearrange("(p t) h d -> p t (h d)", t=TILES)
    k_rows = out_1.rearrange("(p t) h d -> p t (h d)", t=TILES)
    v_rows = out_2.rearrange("(p t) h d -> p t (h d)", t=TILES)

    with ExitStack() as ctx:
        const = ctx.enter_context(tc.tile_pool(name="const", bufs=1))
        x_pool = ctx.enter_context(tc.tile_pool(name="x_pool", bufs=1))
        quant = ctx.enter_context(tc.tile_pool(name="quant", bufs=3))
        work = ctx.enter_context(tc.tile_pool(name="work", bufs=3))
        outs = ctx.enter_context(tc.tile_pool(name="outs", bufs=1))
        psum_t = ctx.enter_context(tc.psum_pool(name="psum_t", bufs=4))
        psum_mx = ctx.enter_context(tc.psum_pool(name="psum_mx", bufs=4))
        ctx.enter_context(tc.manual_schedule())

        w_rows = const.tile([P, 2 * D], BF16)
        cos_sb = const.tile([P, TILES, PAIRS], BF16)
        signed_sin = const.tile([P, 2, TILES, PAIRS], BF16)
        x_tiles = []

        def load_tables(n):
            tiles = slice(sum(TABLE_TILES[:n]), sum(TABLE_TILES[: n + 1]))
            nc.sync.dma_start(out=signed_sin[:, 1, tiles, :], in_=sin_rows[:, tiles, :])
            nc.sync.dma_start(out=cos_sb[:, tiles, :], in_=cos_rows[:, tiles, :])

        def load_x(g):
            x_sb = x_pool.tile([P, GROUP_TILES[g] * D], BF16, name="x_sb", tag="x_%d" % g)
            first = FIRST_TILE[g] * D
            nc.sync.dma_start(out=x_sb[:], in_=x_rows[:, first : first + GROUP_TILES[g] * D])
            x_tiles.append(x_sb)

        for g in range(N_GROUPS):
            load_x(g)
            if g == 0:
                nc.sync.dma_start(
                    out=w_rows[:].rearrange("p (a k) -> p a k", a=2),
                    in_=wqkv.rearrange("(a p) k -> p a k", p=P),
                )
                load_tables(0)
            if g == 3:
                load_tables(1)
            if g == 6:
                load_tables(2)

        ident = const.tile([P, P], F32)
        make_identity(nc, ident[:])

        w_codes = const.tile([P, OUT_COLS], U32, align_bytes=64)
        w_scales = const.tile([P, OUT_COLS], U8, align_bytes=64)

        halves_of = {}
        banks_t = {}
        grouped_of = {}
        codes_of = {}
        banks_of = {}
        out_tiles = {}
        products_of = {}

        def negate_sin(g):
            if FIRST_TILE[g] >= TABLE_TILES[0]:
                tiles = slice(FIRST_TILE[g], FIRST_TILE[g] + GROUP_TILES[g])
                nc.scalar.activation(
                    out=signed_sin[:, 0, tiles, :],
                    in_=signed_sin[:, 1, tiles, :],
                    func=COPY,
                    scale=-1.0,
                )

        def banks_in(g):
            return range(GROUP_TILES[g] // BANK)

        def split_tiles(g):
            return SPLIT_TILES if g >= FIRST_SPLIT and GROUP_TILES[g] == MAX_GROUP else 0

        def split_group(g):
            n_tiles = split_tiles(g)
            if n_tiles:
                halves = quant.tile([P, SPLIT_TILES, 2, P], F32, name="halves")
                nc.scalar.copy(
                    out=halves[:],
                    in_=x_tiles[g][:, 0 : n_tiles * D]
                    .bitcast(F32)
                    .rearrange("p (j w u) -> p j u w", j=n_tiles, u=2),
                )
                halves_of[g] = halves

        def transpose_bank(g, n):
            x_words = x_tiles[g][:].bitcast(F32)
            bank_t = psum_t.tile([P, BANK, 2, P], F32, tag="bank_t", name="bank_t")
            for j in range(BANK):
                tile = BANK * n + j
                if tile < split_tiles(g):
                    for u in range(2):
                        nc.tensor.transpose(
                            bank_t[:, j, u, :], halves_of[g][:, tile, u, :], ident[:]
                        )
                else:
                    transpose_rows(nc, bank_t, j, x_words, tile * WORDS, ident)
            banks_t[(g, n)] = bank_t

        def interleave_group(g, copy):
            grouped = quant.tile([P, MAX_GROUP * P * 4], BF16, align_bytes=64, name="grouped")
            words = grouped[:].bitcast(F32).rearrange("p (j r u) -> p j r u", r=P, u=2)
            for n in banks_in(g):
                copy(
                    out=words[:, BANK * n : BANK * (n + 1), :, :],
                    in_=banks_t[(g, n)][:].rearrange("p j u r -> p j r u"),
                )
            grouped_of[g] = grouped

        def quantise_group(g):
            cols = GROUP_TILES[g] * P
            codes = quant.tile([P, MAX_GROUP * P], U32, align_bytes=64, name="codes")
            scales = quant.tile([P, MAX_GROUP * P], U8, align_bytes=64, name="scales")
            nc.vector.quantize_mx(
                out=codes[:, 0:cols].bitcast(FP8X4),
                scales=scales[:, 0:cols],
                in_=grouped_of[g][:, 0 : 4 * cols],
            )
            codes_of[g] = (codes, scales)

        def multiply_bank(g, n):
            codes, scales = codes_of[g]
            bank = psum_mx.tile([P, BANK, OUT_COLS], F32, tag="bank_mx", name="bank_mx")
            for j in range(BANK):
                rows = slice((BANK * n + j) * P, (BANK * n + j + 1) * P)
                nc.tensor.matmul_mx(
                    out=bank[:, j, :],
                    lhsT=codes[:, rows].bitcast(FP8X4),
                    lhsT_scale=scales[:, rows],
                    rhs=w_codes[:].bitcast(FP8X4),
                    rhs_scale=w_scales[:],
                    start=True,
                    stop=True,
                )
            banks_of[(g, n)] = bank

        def place_of(tile):
            n_set = sum(end <= tile for end in STORE_END)
            return n_set, tile - (STORE_END[n_set] - STORE_TILES[n_set])

        def copy_v(g):
            n_set, first = place_of(FIRST_TILE[g])
            if first == 0:
                size = STORE_TILES[n_set]
                q_sb = outs.tile([P, size, 2 * HEAD], F32, name="q_sb", tag="q_%d" % n_set)
                k_sb = outs.tile([P, size, HEAD], F32, name="k_sb", tag="k_%d" % n_set)
                v_sb = outs.tile([P, size, HEAD], F32, name="v_sb", tag="v_%d" % n_set)
                out_tiles[n_set] = (q_sb, k_sb, v_sb)
            for n in banks_in(g):
                nc.scalar.copy(
                    out=out_tiles[n_set][2][:, first + BANK * n : first + BANK * (n + 1), :],
                    in_=banks_of[(g, n)][:, :, ROPE_COLS:OUT_COLS],
                )

        def multiply_tables(g):
            by_cos = work.tile([P, MAX_GROUP, ROPE_COLS], F32, name="by_cos")
            by_sin = work.tile([P, MAX_GROUP, ROPE_COLS], F32, name="by_sin")
            shape = [P, ROPE_HEADS, BANK, PAIRS, 2]
            for n in banks_in(g):
                here = slice(BANK * n, BANK * (n + 1))
                tiles = slice(FIRST_TILE[g] + BANK * n, FIRST_TILE[g] + BANK * (n + 1))
                pairs = banks_of[(g, n)][:, :, 0:ROPE_COLS].rearrange(
                    "p j (h i f) -> p h j i f", h=ROPE_HEADS, f=2
                )
                for out_sb, table in (
                    (by_cos, cos_sb[:, tiles, :].unsqueeze(1).unsqueeze(4)),
                    (
                        by_sin,
                        signed_sin[:, :, tiles, :]
                        .rearrange("p f t i -> p t i f")[:, :, :, ::-1]
                        .unsqueeze(1),
                    ),
                ):
                    nc.vector.tensor_tensor(
                        out=out_sb[:, here, :].rearrange(
                            "p j (h i f) -> p h j i f", h=ROPE_HEADS, f=2
                        ),
                        in0=pairs,
                        in1=table.to_broadcast(shape),
                        op=MULT,
                    )
            products_of[g] = (by_cos, by_sin)

        def add_heads(engine, g, kind):
            by_cos, by_sin = products_of[g]
            size = GROUP_TILES[g]
            n_set, first = place_of(FIRST_TILE[g])
            cols = (slice(0, 2 * HEAD), slice(2 * HEAD, ROPE_COLS))[kind]
            engine.tensor_tensor(
                out=out_tiles[n_set][kind][:, first : first + size, :].rearrange(
                    "p j (c f) -> p j c f", f=2
                ),
                in0=by_cos[:, 0:size, cols].rearrange("p j (c f) -> p j c f", f=2),
                in1=by_sin[:, 0:size, cols].rearrange("p j (c f) -> p j c f", f=2)[:, :, :, ::-1],
                op=ADD,
            )

        def store_group(g):
            n_set, first = place_of(FIRST_TILE[g])
            if first + GROUP_TILES[g] == STORE_TILES[n_set]:
                q_sb, k_sb, v_sb = out_tiles[n_set]
                tiles = slice(STORE_END[n_set] - STORE_TILES[n_set], STORE_END[n_set])
                nc.sync.dma_start(out=v_rows[:, tiles, :], in_=v_sb[:])
                nc.sync.dma_start(out=q_rows[:, tiles, :], in_=q_sb[:])
                nc.sync.dma_start(out=k_rows[:, tiles, :], in_=k_sb[:])

        w_words = w_rows[:].bitcast(F32)
        w_grouped = const.tile([P, OUT_COLS * 4], BF16, align_bytes=64)
        w_cols = w_grouped[:].bitcast(F32).rearrange("p (c u) -> p c u", u=2)
        w_banks = []
        transpose_bank(0, 0)
        for a in range(2):
            w_bank = psum_t.tile([P, BANK, 2, P], F32, tag="bank_t", name="bank_t")
            transpose_rows(nc, w_bank, 0, w_words, a * WORDS, ident)
            w_banks.append(w_bank[:, 0, :, :].rearrange("p u r -> p r u"))
        transpose_bank(1, 0)
        interleave_group(0, nc.scalar.copy)
        nc.vector.tensor_copy(out=w_cols[:, 0:P, :], in_=w_banks[0])
        nc.scalar.copy(out=w_cols[:, P : 2 * P, :], in_=w_banks[1])
        quantise_group(0)
        nc.vector.quantize_mx(out=w_codes[:].bitcast(FP8X4), scales=w_scales[:], in_=w_grouped[:])
        interleave_group(1, nc.vector.tensor_copy)
        nc.vector.tensor_scalar_mul(
            out=signed_sin[:, 0, 0 : TABLE_TILES[0], :],
            in0=signed_sin[:, 1, 0 : TABLE_TILES[0], :],
            scalar1=-1.0,
        )
        quantise_group(1)
        for g in range(N_GROUPS + 1):
            if g < N_GROUPS:
                for n in banks_in(g):
                    multiply_bank(g, n)
            if g + 2 < N_GROUPS:
                for n in banks_in(g + 2):
                    transpose_bank(g + 2, n)
            if 1 <= g < N_GROUPS - 1:
                interleave_group(g + 1, nc.scalar.copy)
            if g + 2 < N_GROUPS:
                negate_sin(g + 2)
            if g + 3 < N_GROUPS:
                split_group(g + 3)
            if g == N_GROUPS - 1:
                copy_v(g)
            if g >= 1:
                multiply_tables(g - 1)
            if 1 <= g < N_GROUPS:
                copy_v(g - 1)
            if 2 <= g:
                add_heads(nc.vector, g - 2, 1)
                store_group(g - 2)
            if 1 <= g < N_GROUPS - 1:
                quantise_group(g + 1)
            if 1 <= g < N_GROUPS:
                add_heads(nc.gpsimd, g - 1, 0)
        add_heads(nc.vector, N_GROUPS - 1, 0)
        add_heads(nc.vector, N_GROUPS - 1, 1)
        store_group(N_GROUPS - 1)
